import numpy as np
import ml_dtypes


def mxq(x, axis, fmt="e4m3"):
    dtype, down = {"e4m3": (ml_dtypes.float8_e4m3fn, 7), "e5m2": (ml_dtypes.float8_e5m2, 14)}[fmt]
    v = np.moveaxis(np.asarray(x, np.float32).astype(ml_dtypes.bfloat16).astype(np.float64), axis, -1)
    blocks = v.reshape(v.shape[:-1] + (-1, 32))
    amax = np.abs(blocks).max(-1, keepdims=True)
    byte = np.maximum(np.where(amax > 0, np.frexp(amax)[1] - 1 + 127, 0) - down, 1)
    scale = np.exp2(byte - 127.0)
    codes = (blocks / scale).astype(np.float32).astype(dtype).astype(np.float64)
    return np.moveaxis((codes * scale).reshape(v.shape), -1, axis)


WIDE = False


def mx_kscale(k):
    if not WIDE:
        return np.ones(k)
    levels = np.array([10, -10, 5, -5, 0])
    if k % 512:
        return np.exp2(np.random.permutation(np.resize(levels, k // 32))).repeat(32)
    a = np.empty((k // 512, 16))
    for p in range(k // 512):
        a[p, :8] = np.random.permutation(np.resize(levels, 8))
        for g in range(8):
            far = levels[np.abs(levels - a[p, g]) >= 10]
            a[p, g + 8] = far[np.random.randint(len(far))]
    return np.exp2(a.ravel()).repeat(32)


BF16 = ml_dtypes.bfloat16


def bf(x):
    return np.asarray(x, np.float32).astype(BF16)


def f64(x):
    return np.asarray(x).astype(np.float64)


B, HEAD, NUM_EXPERTS, HEAD_DIM = 1024, 2, 3, 512
EPS = 1e-5
VAR0 = 3e-4


def sigmoid(v):
    return 1.0 / (1.0 + np.exp(-v))


def pre_activation(x1, x2, x3, W, b):
    n = x1.shape[0]
    xs = np.stack([f64(x1).reshape(n, HEAD, HEAD_DIM),
                   f64(x2).reshape(n, HEAD, HEAD_DIM),
                   f64(x3).reshape(n, HEAD, HEAD_DIM)], axis=2)
    y = xs.transpose(1, 2, 0, 3) @ f64(W).transpose(0, 1, 3, 2)
    y = y.transpose(2, 1, 0, 3) + f64(b).transpose(1, 0, 2)
    return y.reshape(n, NUM_EXPERTS * HEAD * HEAD_DIM)


def setup_inputs():
    s = mx_kscale(B)[:, None]
    u = mx_kscale(HEAD_DIM)
    p = (HEAD, NUM_EXPERTS, HEAD_DIM)
    x10 = bf(np.random.standard_normal((B, HEAD * HEAD_DIM)))
    x20 = bf(np.random.standard_normal((B, HEAD * HEAD_DIM)))
    x30 = bf(np.random.standard_normal((B, HEAD * HEAD_DIM)))
    W0 = bf(np.random.standard_normal((HEAD, NUM_EXPERTS, HEAD_DIM, HEAD_DIM)) / np.sqrt(HEAD_DIM))
    b = bf(np.random.standard_normal(p) * 0.3)
    gamma = bf(np.sqrt(VAR0) * (1.0 + 0.1 * np.random.standard_normal(p)))
    beta = bf(np.random.standard_normal(p) * 0.3)
    running_mean = bf(np.random.standard_normal(p) * 0.3)
    running_var = bf(VAR0 * np.random.uniform(0.5, 1.5, p))
    g = (np.random.standard_normal((B, NUM_EXPERTS * HEAD * HEAD_DIM)) * 4.0
         * np.exp2(np.random.randint(-6, 1, (B, 1))) / s)
    g = bf((g.reshape(B, NUM_EXPERTS * HEAD, HEAD_DIM) * u).reshape(B, NUM_EXPERTS * HEAD * HEAD_DIM))
    y = pre_activation(x10, x20, x30, W0, b)
    return {"x1": bf(f64(x10) * s), "x2": bf(f64(x20) * s), "x3": bf(f64(x30) * s),
            "W": bf(f64(W0) / u[:, None]), "b": b, "gamma": gamma, "beta": beta,
            "running_mean": running_mean, "running_var": running_var,
            "y": np.asarray(y, np.float32), "grad_out": g}


def reference(x1, x2, x3, W, b, gamma, beta, running_mean, running_var, y, grad_out):
    n = x1.shape[0]
    xs = np.stack([f64(x1).reshape(n, HEAD, HEAD_DIM),
                   f64(x2).reshape(n, HEAD, HEAD_DIM),
                   f64(x3).reshape(n, HEAD, HEAD_DIM)], axis=2)
    yf = f64(y).reshape(n, NUM_EXPERTS, HEAD, HEAD_DIM)
    g = f64(grad_out).reshape(n, NUM_EXPERTS, HEAD, HEAD_DIM)
    c = (f64(gamma) * (1.0 / np.sqrt(f64(running_var) + EPS))).transpose(1, 0, 2)
    sg = sigmoid(1.702 * yf)
    dy = g * c * (sg * (1.0 + 1.702 * yf * (1.0 - sg)))
    d0 = mxq(dy[:, 0], 2, "e5m2")
    w0 = mxq(f64(W)[:, 0], 1, "e4m3")
    dx1 = d0.transpose(1, 0, 2) @ w0
    dx1 = dx1.transpose(1, 0, 2).reshape(n, HEAD * HEAD_DIM)
    dq = mxq(dy, 0, "e5m2")
    xq = mxq(xs, 0, "e4m3")
    dW = dq.transpose(2, 1, 3, 0) @ xq.transpose(1, 2, 0, 3)
    return dx1, dW

@@ -1,0 +1,373 @@
+from contextlib import ExitStack
+
+import concourse.mybir as mybir
+from concourse.masks import make_identity
+
+F32 = mybir.dt.float32
+BF16 = mybir.dt.bfloat16
+U32 = mybir.dt.uint32
+U8 = mybir.dt.uint8
+E4X4 = mybir.dt.float8_e4m3fn_x4
+E5X4 = mybir.dt.float8_e5m2_x4
+ACT = mybir.ActivationFunctionType
+ALU = mybir.AluOpType
+
+P = 128
+J = 4
+FW = 512
+EPS = 1e-5
+
+FLOPS = 2 * 1024 * 512 * 512 * 2 + 6 * 2 * 512 * 512 * 1024
+BYTES = 1024 * 3072 * 4 + 1024 * 3072 * 2 + 3 * 1024 * 1024 * 2 + 2 * 512 * 512 * 2 + 2 * 3072 * 2 + 1024 * 1024 * 4 + 6 * 512 * 512 * 4
+
+
+def tile_mom_v_kernel(tc, x1, x2, x3, W, b, gamma, beta, running_mean, running_var, y, grad_out, out_0, out_1):
+    nc = tc.nc
+    xs = (x1, x2, x3)
+    units = [(e, g, h) for e in range(3) for g in range(2) for h in range(2)]
+    n_units = len(units)
+    w_rows = W.rearrange("h e f d -> (h e f) d")
+    o1_rows = out_1.rearrange("h e f d -> (h e f) d")
+
+    with ExitStack() as ctx:
+        ctx.enter_context(tc.manual_schedule())
+        sb = ctx.enter_context(tc.tile_pool(name="sb", bufs=1))
+        ps = ctx.enter_context(tc.psum_pool(name="ps", bufs=1))
+
+        t_y = {}
+        t_g = {}
+        t_x = {}
+        t_p = {}
+        t_xg = {}
+        t_dyn = {}
+        t_dyi = {}
+        t_g0 = {}
+        t_c0 = {}
+        t_dc = {}
+        t_xc = {}
+        t_cb = {}
+        t_tp = {}
+        t_acc0 = {}
+        t_acc1 = {}
+
+        warm = sb.tile([P, 1], F32, name="warm", tag="warm")
+        warm2 = sb.tile([P, 1], F32, name="warm2", tag="warm2")
+        nc.vector.memset(warm[:], 1.0)
+        nc.scalar.activation(out=warm2[:], in_=warm[:], func=ACT.Sqrt)
+        gam = sb.tile([P, FW], BF16, name="gam", tag="gam")
+        var = sb.tile([P, FW], BF16, name="var", tag="var")
+        nc.vector.memset(gam[:], 0.0)
+        nc.vector.memset(var[:], 0.0)
+        var_rows = running_var.rearrange("h e f -> (h e) f")
+        gam_rows = gamma.rearrange("h e f -> (h e) f")
+        nc.sync.dma_start(out=var[0:4, :], in_=var_rows[0:4, :])
+        nc.sync.dma_start(out=var[4:6, :], in_=var_rows[4:6, :])
+        nc.sync.dma_start(out=gam[0:4, :], in_=gam_rows[0:4, :])
+        nc.sync.dma_start(out=gam[4:6, :], in_=gam_rows[4:6, :])
+        ident = sb.tile([P, P], F32, name="ident", tag="ident")
+        make_identity(nc, ident[:])
+        sd = sb.tile([P, FW], F32, name="sd", tag="sd")
+        rs = sb.tile([P, FW], F32, name="rs", tag="rs")
+        c3 = sb.tile([P, FW], F32, name="c3", tag="c3")
+        nc.scalar.activation(out=sd[:], in_=var[:], func=ACT.Sqrt, bias=EPS, scale=1.0)
+        nc.scalar.activation(out=warm2[:], in_=warm[:], func=ACT.Tanh)
+        nc.vector.reciprocal(out=rs[:], in_=sd[:])
+        nc.vector.scalar_tensor_tensor(out=c3[:], in0=rs[:], scalar=-0.5, in1=gam[:], op0=ALU.mult, op1=ALU.mult)
+
+        w_codes = sb.tile([P, 2, FW], U32, name="w_codes", tag="w_codes", align_bytes=64)
+        w_scales = sb.tile([P, 2, FW], U8, name="w_scales", tag="w_scales", align_bytes=64)
+        t_w = {}
+
+        def spread_c(c):
+            e, h = c // 2, c % 2
+            r = 3 * h + e
+            cb = ps.tile([P, FW], F32, name="cb", tag="cb", bufs=2)
+            nc.tensor.matmul(out=cb[:], lhsT=ident[:, r : r + 1].to_broadcast([P, P]), rhs=c3[:], start=True, stop=True)
+            t_cb[c] = cb
+
+        def load(u):
+            e, g, h = units[u]
+            r0 = 512 * g
+            c0 = 512 * (2 * e + h)
+            first = e == 0 and g == 0
+            g_src = grad_out[r0 : r0 + 512, 1024 * e : 1024 * e + 1024].rearrange("(p j) w -> p j w", j=J)
+            x_src = xs[e][r0 : r0 + 512, :].rearrange("(p j) w -> p j w", j=J)
+            y_src = y[r0 : r0 + 512, c0 : c0 + 512].rearrange("(p j) w -> p j w", j=J)
+            hs = slice(512 * h, 512 * h + 512)
+            if h == 0:
+                gt = sb.tile([P, J, 2 * FW], BF16, name="g_raw", tag="g_raw", bufs=3)
+                t_g[(e, g)] = gt
+                xt = sb.tile([P, J, 2 * FW], BF16, name="x_raw", tag="x_raw", bufs=2)
+                t_x[(e, g)] = xt
+            yt = sb.tile([P, J, FW], F32, name="y_raw", tag="y_raw", bufs=5)
+            t_y[u] = yt
+            if u == 0:
+                nc.sync.dma_start(out=yt[:, 0:1, :], in_=y_src[:, 0:1, :])
+                nc.sync.dma_start(out=t_g[(e, g)][:, :, hs], in_=g_src[:, :, hs])
+                for j in range(1, J):
+                    nc.sync.dma_start(out=yt[:, j : j + 1, :], in_=y_src[:, j : j + 1, :])
+                nc.sync.dma_start(out=t_x[(e, g)][:, :, hs], in_=x_src[:, :, hs])
+            elif first:
+                nc.sync.dma_start(out=yt[:], in_=y_src)
+                nc.sync.dma_start(out=t_g[(e, g)][:, :, hs], in_=g_src[:, :, hs])
+                nc.sync.dma_start(out=t_x[(e, g)][:, :, hs], in_=x_src[:, :, hs])
+            else:
+                if h == 0:
+                    nc.sync.dma_start(out=t_g[(e, g)][:], in_=g_src)
+                nc.sync.dma_start(out=yt[:], in_=y_src)
+                if h == 0:
+                    nc.sync.dma_start(out=t_x[(e, g)][:], in_=x_src)
+
+        def load_w(h):
+            wr = sb.tile([P, J, FW], BF16, name="w_raw", tag="w_raw", bufs=1)
+            f0 = 3 * h * 512
+            nc.sync.dma_start(out=wr[:], in_=w_rows[f0 : f0 + 512, :].rearrange("(q t) d -> q t d", t=J))
+            t_w[h] = wr
+
+        def w_interleave(h):
+            wg = sb.tile([P, FW, J], BF16, name="w_grp", tag="w_grp", bufs=1, align_bytes=64)
+            nc.vector.tensor_copy(out=wg[:], in_=t_w[h][:].rearrange("q t d -> q d t"))
+            t_w[(h, 1)] = wg
+
+        def w_quant(h):
+            nc.vector.quantize_mx(out=w_codes[:, h, :].bitcast(E4X4), scales=w_scales[:, h, :], in_=t_w[(h, 1)][:].rearrange("q d t -> q (d t)"))
+
+        def acts(u):
+            pt = sb.tile([P, J, FW], F32, name="p_t", tag="p_t", bufs=4)
+            yt = t_y[u]
+            step = 1 if u == 0 else J
+            for j in range(0, J, step):
+                nc.scalar.activation(out=pt[:, j : j + step, :], in_=yt[:, j : j + step, :], func=ACT.Tanh, scale=0.851)
+            for j in range(0, J, step):
+                nc.scalar.activation(out=yt[:, j : j + step, :], in_=yt[:, j : j + step, :], func=ACT.Silu, scale=-1.702)
+            t_p[u] = pt
+
+        def x_interleave(u):
+            e, g, h = units[u]
+            xg = sb.tile([P, FW, J], BF16, name="x_grp", tag="x_grp", bufs=2, align_bytes=64)
+            nc.scalar.copy(out=xg[:], in_=t_x[(e, g)][:, :, 512 * h : 512 * h + 512].rearrange("p j w -> p w j"))
+            t_xg[u] = xg
+
+        def v_a(u):
+            e, g, h = units[u]
+            pt = t_p[u]
+            step = 1 if u == 0 else J
+            for j in range(0, J, step):
+                nc.vector.scalar_tensor_tensor(
+                    out=pt[:, j : j + step, :],
+                    in0=pt[:, j : j + step, :],
+                    scalar=1.0,
+                    in1=t_g[(e, g)][:, j : j + step, 512 * h : 512 * h + 512],
+                    op0=ALU.add,
+                    op1=ALU.mult,
+                )
+
+        def v_b(u):
+            nc.vector.scalar_tensor_tensor(out=t_p[u][:], in0=t_y[u][:], scalar=1.0, in1=t_p[u][:], op0=ALU.subtract, op1=ALU.mult)
+
+        def v_d(u):
+            e, g, h = units[u]
+            cb = t_cb[2 * e + h]
+            if e == 0:
+                dyn = sb.tile([P, J, FW], BF16, name="dyn", tag="dyn", bufs=2)
+                nc.vector.tensor_tensor(out=dyn[:], in0=t_p[u][:], in1=cb[:].unsqueeze(1).to_broadcast([P, J, FW]), op=ALU.mult)
+                t_dyn[u] = dyn
+            else:
+                dyi = sb.tile([P, FW, J], BF16, name="dyi", tag="dyi", bufs=3, align_bytes=64)
+                n_part = 2 if u == n_units - 1 else 1
+                fw = FW // n_part
+                for k in range(n_part):
+                    nc.vector.tensor_tensor(
+                        out=dyi[:, k * fw : (k + 1) * fw, :],
+                        in0=t_p[u][:, :, k * fw : (k + 1) * fw].rearrange("p j f -> p f j"),
+                        in1=cb[:, k * fw : (k + 1) * fw].unsqueeze(2).to_broadcast([P, fw, J]),
+                        op=ALU.mult,
+                    )
+                t_dyi[u] = dyi
+
+        def v_i(u):
+            dyi = sb.tile([P, FW, J], BF16, name="dyi", tag="dyi", bufs=3, align_bytes=64)
+            nc.vector.tensor_copy(out=dyi[:], in_=t_dyn[u][:].rearrange("p j f -> p f j"))
+            t_dyi[u] = dyi
+
+        def q_d(u):
+            e, g, h = units[u]
+            c = 2 * e + h
+            if g == 0:
+                dc = sb.tile([P, 2, FW], U32, name="d_codes", tag="d_codes", bufs=3, align_bytes=64)
+                ds = sb.tile([P, 2, FW], U8, name="d_scales", tag="d_scales", bufs=3, align_bytes=64)
+                t_dc[c] = (dc, ds)
+            dc, ds = t_dc[c]
+            n_part = 2 if u == n_units - 1 else 1
+            fw = FW // n_part
+            for k in range(n_part):
+                fs = slice(k * fw, (k + 1) * fw)
+                nc.vector.quantize_mx(out=dc[:, g, fs].bitcast(E5X4), scales=ds[:, g, fs], in_=t_dyi[u][:, fs, :].rearrange("p f j -> p (f j)"))
+
+        def q_x(u):
+            e, g, h = units[u]
+            c = 2 * e + h
+            if g == 0:
+                xc = sb.tile([P, 2, FW], U32, name="x_codes", tag="x_codes", bufs=4, align_bytes=64)
+                xsc = sb.tile([P, 2, FW], U8, name="x_scales", tag="x_scales", bufs=4, align_bytes=64)
+                t_xc[c] = (xc, xsc)
+            xc, xsc = t_xc[c]
+            nc.vector.quantize_mx(out=xc[:, g, :].bitcast(E4X4), scales=xsc[:, g, :], in_=t_xg[u][:].rearrange("p w j -> p (w j)"))
+
+        def t_0(u):
+            words = t_dyn[u][:].rearrange("p j f -> p (j f)").bitcast(F32)
+            banks = []
+            for jp in range(2):
+                tp = ps.tile([P, FW], F32, name="tp", tag="bank", bufs=6)
+                tpv = tp[:].rearrange("q (a v r) -> q a v r", a=2, v=2)
+                for a in range(2):
+                    j = 2 * jp + a
+                    for v in range(2):
+                        nc.tensor.transpose(tpv[:, a, v, :], words[:, 256 * j + v : 256 * (j + 1) : 2], ident[:])
+                banks.append(tp)
+            t_tp[u] = banks
+
+        def c_0(u):
+            g0 = sb.tile([P, FW, J], BF16, name="g0", tag="g0", bufs=2, align_bytes=64)
+            g0w = g0[:].rearrange("q c t -> q (c t)").bitcast(F32).rearrange("q (a r v) -> q a r v", a=4, v=2)
+            for jp in range(2):
+                tpv = t_tp[u][jp][:].rearrange("q (a v r) -> q a r v", a=2, v=2)
+                nc.scalar.copy(out=g0w[:, 2 * jp : 2 * jp + 2, :, :], in_=tpv)
+            t_g0[u] = g0
+
+        def q_0(u):
+            c0 = sb.tile([P, FW], U32, name="c0", tag="c0", bufs=2, align_bytes=64)
+            s0 = sb.tile([P, FW], U8, name="s0", tag="s0", bufs=2, align_bytes=64)
+            nc.vector.quantize_mx(out=c0[:].bitcast(E5X4), scales=s0[:], in_=t_g0[u][:].rearrange("q c t -> q (c t)"))
+            t_c0[u] = (c0, s0)
+
+        def m_0(u):
+            e, g, h = units[u]
+            c0, s0 = t_c0[u]
+            banks = []
+            for j in range(J):
+                acc = ps.tile([P, FW], F32, name="acc0", tag="bank", bufs=6)
+                nc.tensor.matmul_mx(
+                    out=acc[:],
+                    lhsT=c0[:, 128 * j : 128 * j + 128].bitcast(E5X4),
+                    lhsT_scale=s0[:, 128 * j : 128 * j + 128],
+                    rhs=w_codes[:, h, :].bitcast(E4X4),
+                    rhs_scale=w_scales[:, h, :],
+                    start=True,
+                    stop=True,
+                )
+                banks.append(acc)
+            t_acc0[u] = banks
+
+        def e_0(u):
+            e, g, h = units[u]
+            o0 = sb.tile([P, J, FW], F32, name="o0", tag="ost", bufs=2)
+            for j in range(J):
+                nc.scalar.copy(out=o0[:, j, :], in_=t_acc0[u][j][:])
+            nc.sync.dma_start(out=out_0[512 * g : 512 * g + 512, 512 * h : 512 * h + 512].rearrange("(p j) d -> p j d", j=J), in_=o0[:])
+
+        def m_1(c):
+            dc, ds = t_dc[c]
+            xc, xsc = t_xc[c]
+            banks = []
+            for ft in range(4):
+                acc = ps.tile([P, FW], F32, name="acc1", tag="bank", bufs=6)
+                for g in range(2):
+                    nc.tensor.matmul_mx(
+                        out=acc[:],
+                        lhsT=dc[:, g, 128 * ft : 128 * ft + 128].bitcast(E5X4),
+                        lhsT_scale=ds[:, g, 128 * ft : 128 * ft + 128],
+                        rhs=xc[:, g, :].bitcast(E4X4),
+                        rhs_scale=xsc[:, g, :],
+                        start=(g == 0),
+                        stop=(g == 1),
+                    )
+                banks.append(acc)
+            t_acc1[c] = banks
+
+        def e_1(c):
+            e, h = c // 2, c % 2
+            o1 = sb.tile([P, 4, FW], F32, name="o1", tag="ost", bufs=2)
+            f0 = (3 * h + e) * 512
+            dst = o1_rows[f0 : f0 + 512, :].rearrange("(t p) d -> p t d", p=P)
+            if e < 2:
+                for ft in range(4):
+                    nc.scalar.copy(out=o1[:, ft, :], in_=t_acc1[c][ft][:])
+                nc.sync.dma_start(out=dst, in_=o1[:])
+            else:
+                for ft in range(4):
+                    if ft % 2 == 0:
+                        nc.scalar.copy(out=o1[:, ft, :], in_=t_acc1[c][ft][:])
+                    else:
+                        nc.vector.tensor_copy(out=o1[:, ft, :], in_=t_acc1[c][ft][:])
+                    if ft % 2 == 1:
+                        nc.sync.dma_start(out=dst[:, ft - 1 : ft + 1, :], in_=o1[:, ft - 1 : ft + 1, :])
+
+        def is_unit(u):
+            return 0 <= u < n_units
+
+        def qd_iter(u):
+            return u + 4 if units[u][0] == 0 else u + 3
+
+        def expert0(u):
+            return is_unit(u) and units[u][0] == 0
+
+        spread_c(0)
+        spread_c(1)
+        pending_e1 = []
+        for s in range(-3, n_units + 6):
+            if is_unit(s + 3):
+                load(s + 3)
+            if s == -1:
+                load_w(0)
+            if s == 1:
+                load_w(1)
+            for c in range(2, 6):
+                if s == 4 * (c // 2) + (c % 2) + 1:
+                    spread_c(c)
+            if is_unit(s + 1):
+                acts(s + 1)
+                x_interleave(s + 1)
+            if expert0(s - 3):
+                c_0(s - 3)
+            if expert0(s - 5):
+                e_0(s - 5)
+            late_e1 = [c for c in pending_e1 if c >= 4]
+            for c in pending_e1:
+                if c < 4:
+                    e_1(c)
+            pending_e1 = []
+
+            if is_unit(s):
+                v_a(s)
+            if is_unit(s - 1):
+                v_b(s - 1)
+            if is_unit(s):
+                q_x(s)
+            if s == 0:
+                w_interleave(0)
+            if s == 2:
+                w_interleave(1)
+            if is_unit(s - 2):
+                v_d(s - 2)
+                if expert0(s - 2):
+                    t_0(s - 2)
+            if s == 1:
+                w_quant(0)
+            if s == 3:
+                w_quant(1)
+            if expert0(s - 3):
+                v_i(s - 3)
+            for u in range(n_units):
+                if qd_iter(u) == s:
+                    q_d(u)
+            if expert0(s - 4):
+                q_0(s - 4)
+                m_0(s - 4)
+            for u in range(n_units):
+                if qd_iter(u) == s and units[u][1] == 1:
+                    c = 2 * units[u][0] + units[u][2]
+                    m_1(c)
+                    pending_e1.append(c)
+            for c in late_e1:
+                e_1(c)

@@ -21,11 +21,19 @@ FLOPS = 2 * 1024 * 512 * 512 * 2 + 6 * 2 * 512 * 512 * 1024
 BYTES = 1024 * 3072 * 4 + 1024 * 3072 * 2 + 3 * 1024 * 1024 * 2 + 2 * 512 * 512 * 2 + 2 * 3072 * 2 + 1024 * 1024 * 4 + 6 * 512 * 512 * 4
 
 
+XI_S = 512
+XI_G = 0
+VI_ON_S = False
+W_ON_S = False
+FAST = False
+
+
 def tile_mom_v_kernel(tc, x1, x2, x3, W, b, gamma, beta, running_mean, running_var, y, grad_out, out_0, out_1):
     nc = tc.nc
     xs = (x1, x2, x3)
     units = [(e, g, h) for e in range(3) for g in range(2) for h in range(2)]
     n_units = len(units)
+    last = n_units - 1
     w_rows = W.rearrange("h e f d -> (h e f) d")
     o1_rows = out_1.rearrange("h e f d -> (h e f) d")
 
@@ -49,6 +57,8 @@ def tile_mom_v_kernel(tc, x1, x2, x3, W, b, gamma, beta, running_mean, running_v
         t_tp = {}
         t_acc0 = {}
         t_acc1 = {}
+        t_o1 = {}
+        t_w = {}
 
         warm = sb.tile([P, 1], F32, name="warm", tag="warm")
         warm2 = sb.tile([P, 1], F32, name="warm2", tag="warm2")
@@ -56,14 +66,12 @@ def tile_mom_v_kernel(tc, x1, x2, x3, W, b, gamma, beta, running_mean, running_v
         nc.scalar.activation(out=warm2[:], in_=warm[:], func=ACT.Sqrt)
         gam = sb.tile([P, FW], BF16, name="gam", tag="gam")
         var = sb.tile([P, FW], BF16, name="var", tag="var")
-        nc.vector.memset(gam[:], 0.0)
         nc.vector.memset(var[:], 0.0)
+        nc.vector.memset(gam[:], 0.0)
         var_rows = running_var.rearrange("h e f -> (h e) f")
         gam_rows = gamma.rearrange("h e f -> (h e) f")
         nc.sync.dma_start(out=var[0:4, :], in_=var_rows[0:4, :])
         nc.sync.dma_start(out=var[4:6, :], in_=var_rows[4:6, :])
-        nc.sync.dma_start(out=gam[0:4, :], in_=gam_rows[0:4, :])
-        nc.sync.dma_start(out=gam[4:6, :], in_=gam_rows[4:6, :])
         ident = sb.tile([P, P], F32, name="ident", tag="ident")
         make_identity(nc, ident[:])
         sd = sb.tile([P, FW], F32, name="sd", tag="sd")
@@ -71,12 +79,27 @@ def tile_mom_v_kernel(tc, x1, x2, x3, W, b, gamma, beta, running_mean, running_v
         c3 = sb.tile([P, FW], F32, name="c3", tag="c3")
         nc.scalar.activation(out=sd[:], in_=var[:], func=ACT.Sqrt, bias=EPS, scale=1.0)
         nc.scalar.activation(out=warm2[:], in_=warm[:], func=ACT.Tanh)
-        nc.vector.reciprocal(out=rs[:], in_=sd[:])
-        nc.vector.scalar_tensor_tensor(out=c3[:], in0=rs[:], scalar=-0.5, in1=gam[:], op0=ALU.mult, op1=ALU.mult)
 
         w_codes = sb.tile([P, 2, FW], U32, name="w_codes", tag="w_codes", align_bytes=64)
         w_scales = sb.tile([P, 2, FW], U8, name="w_scales", tag="w_scales", align_bytes=64)
-        t_w = {}
+
+        def interleave(eng, dst, src):
+            if FAST:
+                d = dst.rearrange("p (c i) t -> p c t i", i=4)
+                s_ = src.rearrange("p t (c i) -> p c t i", i=4)
+            else:
+                d = dst
+                s_ = src.rearrange("p t c -> p c t")
+            if eng == "S":
+                nc.scalar.copy(out=d, in_=s_)
+            elif eng == "V":
+                nc.vector.tensor_copy(out=d, in_=s_)
+            else:
+                nc.gpsimd.tensor_scalar(out=d, in0=s_, scalar1=1.0, scalar2=0.0, op0=ALU.mult, op1=ALU.add)
+
+        def make_c3():
+            nc.vector.reciprocal(out=rs[:], in_=sd[:])
+            nc.vector.scalar_tensor_tensor(out=c3[:], in0=rs[:], scalar=-0.5, in1=gam[:], op0=ALU.mult, op1=ALU.mult)
 
         def spread_c(c):
             e, h = c // 2, c % 2
@@ -91,81 +114,91 @@ def tile_mom_v_kernel(tc, x1, x2, x3, W, b, gamma, beta, running_mean, running_v
             c0 = 512 * (2 * e + h)
             first = e == 0 and g == 0
             g_src = grad_out[r0 : r0 + 512, 1024 * e : 1024 * e + 1024].rearrange("(p j) w -> p j w", j=J)
-            x_src = xs[e][r0 : r0 + 512, :].rearrange("(p j) w -> p j w", j=J)
             y_src = y[r0 : r0 + 512, c0 : c0 + 512].rearrange("(p j) w -> p j w", j=J)
             hs = slice(512 * h, 512 * h + 512)
             if h == 0:
                 gt = sb.tile([P, J, 2 * FW], BF16, name="g_raw", tag="g_raw", bufs=3)
                 t_g[(e, g)] = gt
-                xt = sb.tile([P, J, 2 * FW], BF16, name="x_raw", tag="x_raw", bufs=2)
-                t_x[(e, g)] = xt
-            yt = sb.tile([P, J, FW], F32, name="y_raw", tag="y_raw", bufs=5)
+            yt = sb.tile([P, J, FW], F32, name="y_raw", tag="y_raw", bufs=4)
             t_y[u] = yt
             if u == 0:
                 nc.sync.dma_start(out=yt[:, 0:1, :], in_=y_src[:, 0:1, :])
+                nc.sync.dma_start(out=yt[:, 1:2, :], in_=y_src[:, 1:2, :])
                 nc.sync.dma_start(out=t_g[(e, g)][:, :, hs], in_=g_src[:, :, hs])
-                for j in range(1, J):
-                    nc.sync.dma_start(out=yt[:, j : j + 1, :], in_=y_src[:, j : j + 1, :])
-                nc.sync.dma_start(out=t_x[(e, g)][:, :, hs], in_=x_src[:, :, hs])
+                nc.sync.dma_start(out=yt[:, 2:4, :], in_=y_src[:, 2:4, :])
+                nc.sync.dma_start(out=gam[0:4, :], in_=gam_rows[0:4, :])
+                nc.sync.dma_start(out=gam[4:6, :], in_=gam_rows[4:6, :])
             elif first:
                 nc.sync.dma_start(out=yt[:], in_=y_src)
                 nc.sync.dma_start(out=t_g[(e, g)][:, :, hs], in_=g_src[:, :, hs])
-                nc.sync.dma_start(out=t_x[(e, g)][:, :, hs], in_=x_src[:, :, hs])
             else:
                 if h == 0:
                     nc.sync.dma_start(out=t_g[(e, g)][:], in_=g_src)
                 nc.sync.dma_start(out=yt[:], in_=y_src)
-                if h == 0:
-                    nc.sync.dma_start(out=t_x[(e, g)][:], in_=x_src)
+
+        def load_x(u):
+            e, g, h = units[u]
+            if h == 0:
+                r0 = 512 * g
+                xt = sb.tile([P, J, 2 * FW], BF16, name="x_raw", tag="x_raw", bufs=2)
+                nc.sync.dma_start(out=xt[:], in_=xs[e][r0 : r0 + 512, :].rearrange("(p j) w -> p j w", j=J))
+                t_x[(e, g)] = xt
 
         def load_w(h):
-            wr = sb.tile([P, J, FW], BF16, name="w_raw", tag="w_raw", bufs=1)
+            wr = sb.tile([P, J, FW], BF16, name="w_raw", tag="w_raw", bufs=2)
             f0 = 3 * h * 512
             nc.sync.dma_start(out=wr[:], in_=w_rows[f0 : f0 + 512, :].rearrange("(q t) d -> q t d", t=J))
             t_w[h] = wr
 
         def w_interleave(h):
-            wg = sb.tile([P, FW, J], BF16, name="w_grp", tag="w_grp", bufs=1, align_bytes=64)
-            nc.vector.tensor_copy(out=wg[:], in_=t_w[h][:].rearrange("q t d -> q d t"))
+            wg = sb.tile([P, FW, J], BF16, name="w_grp", tag="w_grp", bufs=2, align_bytes=64)
+            interleave("S" if W_ON_S else "V", wg[:], t_w[h][:])
             t_w[(h, 1)] = wg
 
         def w_quant(h):
             nc.vector.quantize_mx(out=w_codes[:, h, :].bitcast(E4X4), scales=w_scales[:, h, :], in_=t_w[(h, 1)][:].rearrange("q d t -> q (d t)"))
 
+        def slices(u):
+            return [(0, 1), (1, 2), (2, 4)] if u == 0 else [(0, J)]
+
         def acts(u):
-            pt = sb.tile([P, J, FW], F32, name="p_t", tag="p_t", bufs=4)
+            pt = sb.tile([P, J, FW], F32, name="p_t", tag="p_t", bufs=3)
             yt = t_y[u]
-            step = 1 if u == 0 else J
-            for j in range(0, J, step):
-                nc.scalar.activation(out=pt[:, j : j + step, :], in_=yt[:, j : j + step, :], func=ACT.Tanh, scale=0.851)
-            for j in range(0, J, step):
-                nc.scalar.activation(out=yt[:, j : j + step, :], in_=yt[:, j : j + step, :], func=ACT.Silu, scale=-1.702)
+            for a, z in slices(u):
+                nc.scalar.activation(out=pt[:, a:z, :], in_=yt[:, a:z, :], func=ACT.Tanh, scale=0.851)
+            for a, z in slices(u):
+                nc.scalar.activation(out=yt[:, a:z, :], in_=yt[:, a:z, :], func=ACT.Silu, scale=-1.702)
             t_p[u] = pt
 
-        def x_interleave(u):
-            e, g, h = units[u]
+        def x_alloc(u):
             xg = sb.tile([P, FW, J], BF16, name="x_grp", tag="x_grp", bufs=2, align_bytes=64)
-            nc.scalar.copy(out=xg[:], in_=t_x[(e, g)][:, :, 512 * h : 512 * h + 512].rearrange("p j w -> p w j"))
             t_xg[u] = xg
+
+        def x_interleave(u, eng):
+            e, g, h = units[u]
+            lo, hi = {"S": (0, XI_S), "G": (XI_S, XI_S + XI_G), "V": (XI_S + XI_G, FW)}[eng]
+            if hi > lo:
+                interleave(eng, t_xg[u][:, lo:hi, :], t_x[(e, g)][:, :, 512 * h + lo : 512 * h + hi])
 
         def v_a(u):
             e, g, h = units[u]
             pt = t_p[u]
-            step = 1 if u == 0 else J
-            for j in range(0, J, step):
+            for a, z in slices(u):
                 nc.vector.scalar_tensor_tensor(
-                    out=pt[:, j : j + step, :],
-                    in0=pt[:, j : j + step, :],
-                    scalar=1.0,
-                    in1=t_g[(e, g)][:, j : j + step, 512 * h : 512 * h + 512],
-                    op0=ALU.add,
-                    op1=ALU.mult,
+                    out=pt[:, a:z, :], in0=pt[:, a:z, :], scalar=1.0, in1=t_g[(e, g)][:, a:z, 512 * h : 512 * h + 512], op0=ALU.add, op1=ALU.mult
                 )
 
         def v_b(u):
-            nc.vector.scalar_tensor_tensor(out=t_p[u][:], in0=t_y[u][:], scalar=1.0, in1=t_p[u][:], op0=ALU.subtract, op1=ALU.mult)
+            for a, z in slices(u):
+                nc.vector.scalar_tensor_tensor(
+                    out=t_p[u][:, a:z, :], in0=t_y[u][:, a:z, :], scalar=1.0, in1=t_p[u][:, a:z, :], op0=ALU.subtract, op1=ALU.mult
+                )
 
-        def v_d(u):
+        def d_alloc(u):
+            dyi = sb.tile([P, FW, J], BF16, name="dyi", tag="dyi", bufs=3, align_bytes=64)
+            t_dyi[u] = dyi
+
+        def v_d(u, lo=0, hi=FW):
             e, g, h = units[u]
             cb = t_cb[2 * e + h]
             if e == 0:
@@ -173,24 +206,18 @@ def tile_mom_v_kernel(tc, x1, x2, x3, W, b, gamma, beta, running_mean, running_v
                 nc.vector.tensor_tensor(out=dyn[:], in0=t_p[u][:], in1=cb[:].unsqueeze(1).to_broadcast([P, J, FW]), op=ALU.mult)
                 t_dyn[u] = dyn
             else:
-                dyi = sb.tile([P, FW, J], BF16, name="dyi", tag="dyi", bufs=3, align_bytes=64)
-                n_part = 2 if u == n_units - 1 else 1
-                fw = FW // n_part
-                for k in range(n_part):
-                    nc.vector.tensor_tensor(
-                        out=dyi[:, k * fw : (k + 1) * fw, :],
-                        in0=t_p[u][:, :, k * fw : (k + 1) * fw].rearrange("p j f -> p f j"),
-                        in1=cb[:, k * fw : (k + 1) * fw].unsqueeze(2).to_broadcast([P, fw, J]),
-                        op=ALU.mult,
-                    )
-                t_dyi[u] = dyi
+                nc.vector.tensor_tensor(
+                    out=t_dyi[u][:, lo:hi, :],
+                    in0=t_p[u][:, :, lo:hi].rearrange("p j f -> p f j"),
+                    in1=cb[:, lo:hi].unsqueeze(2).to_broadcast([P, hi - lo, J]),
+                    op=ALU.mult,
+                )
 
         def v_i(u):
-            dyi = sb.tile([P, FW, J], BF16, name="dyi", tag="dyi", bufs=3, align_bytes=64)
-            nc.vector.tensor_copy(out=dyi[:], in_=t_dyn[u][:].rearrange("p j f -> p f j"))
-            t_dyi[u] = dyi
+            d_alloc(u)
+            interleave("S" if VI_ON_S else "V", t_dyi[u][:], t_dyn[u][:])
 
-        def q_d(u):
+        def q_d(u, lo=0, hi=FW):
             e, g, h = units[u]
             c = 2 * e + h
             if g == 0:
@@ -198,11 +225,7 @@ def tile_mom_v_kernel(tc, x1, x2, x3, W, b, gamma, beta, running_mean, running_v
                 ds = sb.tile([P, 2, FW], U8, name="d_scales", tag="d_scales", bufs=3, align_bytes=64)
                 t_dc[c] = (dc, ds)
             dc, ds = t_dc[c]
-            n_part = 2 if u == n_units - 1 else 1
-            fw = FW // n_part
-            for k in range(n_part):
-                fs = slice(k * fw, (k + 1) * fw)
-                nc.vector.quantize_mx(out=dc[:, g, fs].bitcast(E5X4), scales=ds[:, g, fs], in_=t_dyi[u][:, fs, :].rearrange("p f j -> p (f j)"))
+            nc.vector.quantize_mx(out=dc[:, g, lo:hi].bitcast(E5X4), scales=ds[:, g, lo:hi], in_=t_dyi[u][:, lo:hi, :].rearrange("p f j -> p (f j)"))
 
         def q_x(u):
             e, g, h = units[u]
@@ -266,108 +289,136 @@ def tile_mom_v_kernel(tc, x1, x2, x3, W, b, gamma, beta, running_mean, running_v
                 nc.scalar.copy(out=o0[:, j, :], in_=t_acc0[u][j][:])
             nc.sync.dma_start(out=out_0[512 * g : 512 * g + 512, 512 * h : 512 * h + 512].rearrange("(p j) d -> p j d", j=J), in_=o0[:])
 
-        def m_1(c):
+        def m_1(c, ft):
             dc, ds = t_dc[c]
             xc, xsc = t_xc[c]
-            banks = []
-            for ft in range(4):
-                acc = ps.tile([P, FW], F32, name="acc1", tag="bank", bufs=6)
-                for g in range(2):
-                    nc.tensor.matmul_mx(
-                        out=acc[:],
-                        lhsT=dc[:, g, 128 * ft : 128 * ft + 128].bitcast(E5X4),
-                        lhsT_scale=ds[:, g, 128 * ft : 128 * ft + 128],
-                        rhs=xc[:, g, :].bitcast(E4X4),
-                        rhs_scale=xsc[:, g, :],
-                        start=(g == 0),
-                        stop=(g == 1),
-                    )
-                banks.append(acc)
-            t_acc1[c] = banks
+            acc = ps.tile([P, FW], F32, name="acc1", tag="bank", bufs=6)
+            for g in range(2):
+                nc.tensor.matmul_mx(
+                    out=acc[:],
+                    lhsT=dc[:, g, 128 * ft : 128 * ft + 128].bitcast(E5X4),
+                    lhsT_scale=ds[:, g, 128 * ft : 128 * ft + 128],
+                    rhs=xc[:, g, :].bitcast(E4X4),
+                    rhs_scale=xsc[:, g, :],
+                    start=(g == 0),
+                    stop=(g == 1),
+                )
+            t_acc1[(c, ft)] = acc
+
+        def o1_dst(c):
+            f0 = (3 * (c % 2) + c // 2) * 512
+            return o1_rows[f0 : f0 + 512, :].rearrange("(t p) d -> p t d", p=P)
 
         def e_1(c):
-            e, h = c // 2, c % 2
             o1 = sb.tile([P, 4, FW], F32, name="o1", tag="ost", bufs=2)
-            f0 = (3 * h + e) * 512
-            dst = o1_rows[f0 : f0 + 512, :].rearrange("(t p) d -> p t d", p=P)
-            if e < 2:
-                for ft in range(4):
-                    nc.scalar.copy(out=o1[:, ft, :], in_=t_acc1[c][ft][:])
-                nc.sync.dma_start(out=dst, in_=o1[:])
+            for ft in range(4):
+                nc.scalar.copy(out=o1[:, ft, :], in_=t_acc1[(c, ft)][:])
+            nc.sync.dma_start(out=o1_dst(c), in_=o1[:])
+
+        def e_1_tail(c, ft):
+            if ft == 0:
+                t_o1[c] = sb.tile([P, 4, FW], F32, name="o1", tag="ost", bufs=2)
+            o1 = t_o1[c]
+            if ft % 2 == 0:
+                nc.scalar.copy(out=o1[:, ft, :], in_=t_acc1[(c, ft)][:])
             else:
-                for ft in range(4):
-                    if ft % 2 == 0:
-                        nc.scalar.copy(out=o1[:, ft, :], in_=t_acc1[c][ft][:])
-                    else:
-                        nc.vector.tensor_copy(out=o1[:, ft, :], in_=t_acc1[c][ft][:])
-                    if ft % 2 == 1:
-                        nc.sync.dma_start(out=dst[:, ft - 1 : ft + 1, :], in_=o1[:, ft - 1 : ft + 1, :])
+                nc.vector.tensor_copy(out=o1[:, ft, :], in_=t_acc1[(c, ft)][:])
+            nc.sync.dma_start(out=o1_dst(c)[:, ft : ft + 1, :], in_=o1[:, ft : ft + 1, :])
 
         def is_unit(u):
             return 0 <= u < n_units
 
-        def qd_iter(u):
-            return u + 4 if units[u][0] == 0 else u + 3
-
         def expert0(u):
             return is_unit(u) and units[u][0] == 0
 
-        spread_c(0)
-        spread_c(1)
+        def later(u):
+            return is_unit(u) and units[u][0] > 0
+
+        def chunk_done(u):
+            return 2 * units[u][0] + units[u][2] if units[u][1] == 1 else None
+
         pending_e1 = []
-        for s in range(-3, n_units + 6):
+        for s in range(-3, n_units + 4):
             if is_unit(s + 3):
                 load(s + 3)
-            if s == -1:
+            if is_unit(s + 2):
+                load_x(s + 2)
+            if s == 0:
                 load_w(0)
-            if s == 1:
                 load_w(1)
-            for c in range(2, 6):
-                if s == 4 * (c // 2) + (c % 2) + 1:
-                    spread_c(c)
             if is_unit(s + 1):
                 acts(s + 1)
-                x_interleave(s + 1)
-            if expert0(s - 3):
-                c_0(s - 3)
-            if expert0(s - 5):
-                e_0(s - 5)
-            late_e1 = [c for c in pending_e1 if c >= 4]
+            for c in range(2, 6):
+                if s == 4 * (c // 2) + (c % 2) - 1:
+                    spread_c(c)
+            if is_unit(s):
+                x_alloc(s)
+                x_interleave(s, "S")
+                x_interleave(s, "G")
+            if W_ON_S and s in (1, 2):
+                w_interleave(s - 1)
+            if VI_ON_S and expert0(s - 1):
+                v_i(s - 1)
             for c in pending_e1:
-                if c < 4:
-                    e_1(c)
+                e_1(c)
             pending_e1 = []
+            if expert0(s - 1):
+                c_0(s - 1)
+            if expert0(s - 3):
+                e_0(s - 3)
 
             if is_unit(s):
                 v_a(s)
-            if is_unit(s - 1):
-                v_b(s - 1)
-            if is_unit(s):
-                q_x(s)
             if s == 0:
-                w_interleave(0)
-            if s == 2:
-                w_interleave(1)
-            if is_unit(s - 2):
-                v_d(s - 2)
-                if expert0(s - 2):
-                    t_0(s - 2)
-            if s == 1:
-                w_quant(0)
-            if s == 3:
-                w_quant(1)
-            if expert0(s - 3):
-                v_i(s - 3)
-            for u in range(n_units):
-                if qd_iter(u) == s:
-                    q_d(u)
-            if expert0(s - 4):
-                q_0(s - 4)
-                m_0(s - 4)
-            for u in range(n_units):
-                if qd_iter(u) == s and units[u][1] == 1:
-                    c = 2 * units[u][0] + units[u][2]
-                    m_1(c)
-                    pending_e1.append(c)
-            for c in late_e1:
-                e_1(c)
+                make_c3()
+                spread_c(0)
+                spread_c(1)
+            if expert0(s - 2):
+                q_d(s - 2)
+            if later(s - 1) and s - 1 != last:
+                q_d(s - 1)
+            done = []
+            if expert0(s - 2) and chunk_done(s - 2) is not None:
+                done.append(chunk_done(s - 2))
+            if later(s - 1) and s - 1 != last and chunk_done(s - 1) is not None:
+                done.append(chunk_done(s - 1))
+            if is_unit(s):
+                v_b(s)
+            if is_unit(s):
+                x_interleave(s, "V")
+            if is_unit(s - 1):
+                q_x(s - 1)
+            for c in done:
+                for ft in range(4):
+                    m_1(c, ft)
+                pending_e1.append(c)
+            if s == last:
+                for c in pending_e1:
+                    e_1(c)
+                pending_e1 = []
+                q_x(s)
+                d_alloc(s)
+                for k in range(4):
+                    v_d(s, 128 * k, 128 * k + 128)
+                    if k > 0:
+                        q_d(s, 128 * (k - 1), 128 * k)
+                        m_1(5, k - 1)
+                q_d(s, 384, 512)
+                m_1(5, 3)
+                for ft in range(4):
+                    e_1_tail(5, ft)
+            elif is_unit(s):
+                if later(s):
+                    d_alloc(s)
+                v_d(s)
+                if expert0(s):
+                    t_0(s)
+            if (not W_ON_S) and s in (1, 2):
+                w_interleave(s - 1)
+            if (not VI_ON_S) and expert0(s - 1):
+                v_i(s - 1)
+            if s in (2, 3):
+                w_quant(s - 2)
+            if expert0(s - 2):
+                q_0(s - 2)
+                m_0(s - 2)

@@ -21,11 +21,10 @@ FLOPS = 2 * 1024 * 512 * 512 * 2 + 6 * 2 * 512 * 512 * 1024
 BYTES = 1024 * 3072 * 4 + 1024 * 3072 * 2 + 3 * 1024 * 1024 * 2 + 2 * 512 * 512 * 2 + 2 * 3072 * 2 + 1024 * 1024 * 4 + 6 * 512 * 512 * 4
 
 
-XI_S = 512
-XI_G = 0
+XI_SPLIT = ((512, 0), (512, 0), (512, 0))
 VI_ON_S = False
 W_ON_S = False
-FAST = False
+FAST = True
 
 
 def tile_mom_v_kernel(tc, x1, x2, x3, W, b, gamma, beta, running_mean, running_var, y, grad_out, out_0, out_1):
@@ -176,7 +175,8 @@ def tile_mom_v_kernel(tc, x1, x2, x3, W, b, gamma, beta, running_mean, running_v
 
         def x_interleave(u, eng):
             e, g, h = units[u]
-            lo, hi = {"S": (0, XI_S), "G": (XI_S, XI_S + XI_G), "V": (XI_S + XI_G, FW)}[eng]
+            n_s, n_g = XI_SPLIT[e]
+            lo, hi = {"S": (0, n_s), "G": (n_s, n_s + n_g), "V": (n_s + n_g, FW)}[eng]
             if hi > lo:
                 interleave(eng, t_xg[u][:, lo:hi, :], t_x[(e, g)][:, :, 512 * h + lo : 512 * h + hi])
 
@@ -351,10 +351,10 @@ def tile_mom_v_kernel(tc, x1, x2, x3, W, b, gamma, beta, running_mean, running_v
             for c in range(2, 6):
                 if s == 4 * (c // 2) + (c % 2) - 1:
                     spread_c(c)
-            if is_unit(s):
-                x_alloc(s)
-                x_interleave(s, "S")
-                x_interleave(s, "G")
+            if is_unit(s + 0):
+                x_alloc(s + 0)
+                x_interleave(s + 0, "G")
+                x_interleave(s + 0, "S")
             if W_ON_S and s in (1, 2):
                 w_interleave(s - 1)
             if VI_ON_S and expert0(s - 1):
@@ -384,8 +384,8 @@ def tile_mom_v_kernel(tc, x1, x2, x3, W, b, gamma, beta, running_mean, running_v
                 done.append(chunk_done(s - 1))
             if is_unit(s):
                 v_b(s)
-            if is_unit(s):
-                x_interleave(s, "V")
+            if is_unit(s + 0):
+                x_interleave(s + 0, "V")
             if is_unit(s - 1):
                 q_x(s - 1)
             for c in done:

@@ -24,6 +24,7 @@ BYTES = 1024 * 3072 * 4 + 1024 * 3072 * 2 + 3 * 1024 * 1024 * 2 + 2 * 512 * 512 
 XI_SPLIT = ((512, 0), (512, 0), (512, 0))
 VI_ON_S = False
 W_ON_S = False
+D_G = 128
 FAST = True
 
 
@@ -53,6 +54,7 @@ def tile_mom_v_kernel(tc, x1, x2, x3, W, b, gamma, beta, running_mean, running_v
         t_dc = {}
         t_xc = {}
         t_cb = {}
+        t_cs = {}
         t_tp = {}
         t_acc0 = {}
         t_acc1 = {}
@@ -106,6 +108,11 @@ def tile_mom_v_kernel(tc, x1, x2, x3, W, b, gamma, beta, running_mean, running_v
             cb = ps.tile([P, FW], F32, name="cb", tag="cb", bufs=2)
             nc.tensor.matmul(out=cb[:], lhsT=ident[:, r : r + 1].to_broadcast([P, P]), rhs=c3[:], start=True, stop=True)
             t_cb[c] = cb
+
+        def copy_c(c):
+            cs = sb.tile([P, D_G], F32, name="cb_sb", tag="cb_sb", bufs=3)
+            nc.scalar.copy(out=cs[:], in_=t_cb[c][:, FW - D_G : FW])
+            t_cs[c] = cs
 
         def load(u):
             e, g, h = units[u]
@@ -198,20 +205,30 @@ def tile_mom_v_kernel(tc, x1, x2, x3, W, b, gamma, beta, running_mean, running_v
             dyi = sb.tile([P, FW, J], BF16, name="dyi", tag="dyi", bufs=3, align_bytes=64)
             t_dyi[u] = dyi
 
-        def v_d(u, lo=0, hi=FW):
-            e, g, h = units[u]
-            cb = t_cb[2 * e + h]
-            if e == 0:
-                dyn = sb.tile([P, J, FW], BF16, name="dyn", tag="dyn", bufs=2)
-                nc.vector.tensor_tensor(out=dyn[:], in0=t_p[u][:], in1=cb[:].unsqueeze(1).to_broadcast([P, J, FW]), op=ALU.mult)
-                t_dyn[u] = dyn
+        def d_pass(eng, u, lo, hi, cvals):
+            if units[u][0] == 0:
+                eng.tensor_tensor(
+                    out=t_dyn[u][:, :, lo:hi], in0=t_p[u][:, :, lo:hi], in1=cvals.unsqueeze(1).to_broadcast([P, J, hi - lo]), op=ALU.mult
+                )
             else:
-                nc.vector.tensor_tensor(
+                eng.tensor_tensor(
                     out=t_dyi[u][:, lo:hi, :],
                     in0=t_p[u][:, :, lo:hi].rearrange("p j f -> p f j"),
-                    in1=cb[:, lo:hi].unsqueeze(2).to_broadcast([P, hi - lo, J]),
+                    in1=cvals.unsqueeze(2).to_broadcast([P, hi - lo, J]),
                     op=ALU.mult,
                 )
+
+        def v_d(u, lo=0, hi=FW):
+            e, g, h = units[u]
+            d_pass(nc.vector, u, lo, hi, t_cb[2 * e + h][:, lo:hi])
+
+        def g_d(u):
+            e, g, h = units[u]
+            d_pass(nc.gpsimd, u, FW - D_G, FW, t_cs[2 * e + h][:])
+
+        def dyn_alloc(u):
+            dyn = sb.tile([P, J, FW], BF16, name="dyn", tag="dyn", bufs=2)
+            t_dyn[u] = dyn
 
         def v_i(u):
             d_alloc(u)
@@ -355,6 +372,9 @@ def tile_mom_v_kernel(tc, x1, x2, x3, W, b, gamma, beta, running_mean, running_v
                 x_alloc(s + 0)
                 x_interleave(s + 0, "G")
                 x_interleave(s + 0, "S")
+            for c in range(2, 6):
+                if D_G and s == 4 * (c // 2) + (c % 2) - 1:
+                    copy_c(c)
             if W_ON_S and s in (1, 2):
                 w_interleave(s - 1)
             if VI_ON_S and expert0(s - 1):
@@ -373,6 +393,9 @@ def tile_mom_v_kernel(tc, x1, x2, x3, W, b, gamma, beta, running_mean, running_v
                 make_c3()
                 spread_c(0)
                 spread_c(1)
+                if D_G:
+                    copy_c(0)
+                    copy_c(1)
             if expert0(s - 2):
                 q_d(s - 2)
             if later(s - 1) and s - 1 != last:
@@ -382,8 +405,6 @@ def tile_mom_v_kernel(tc, x1, x2, x3, W, b, gamma, beta, running_mean, running_v
                 done.append(chunk_done(s - 2))
             if later(s - 1) and s - 1 != last and chunk_done(s - 1) is not None:
                 done.append(chunk_done(s - 1))
-            if is_unit(s):
-                v_b(s)
             if is_unit(s + 0):
                 x_interleave(s + 0, "V")
             if is_unit(s - 1):
@@ -392,6 +413,8 @@ def tile_mom_v_kernel(tc, x1, x2, x3, W, b, gamma, beta, running_mean, running_v
                 for ft in range(4):
                     m_1(c, ft)
                 pending_e1.append(c)
+            if is_unit(s):
+                v_b(s)
             if s == last:
                 for c in pending_e1:
                     e_1(c)
@@ -410,7 +433,11 @@ def tile_mom_v_kernel(tc, x1, x2, x3, W, b, gamma, beta, running_mean, running_v
             elif is_unit(s):
                 if later(s):
                     d_alloc(s)
-                v_d(s)
+                else:
+                    dyn_alloc(s)
+                if D_G:
+                    g_d(s)
+                v_d(s, 0, FW - D_G)
                 if expert0(s):
                     t_0(s)
             if (not W_ON_S) and s in (1, 2):

@@ -7,445 +7,431 @@ F32 = mybir.dt.float32
 BF16 = mybir.dt.bfloat16
 U32 = mybir.dt.uint32
 U8 = mybir.dt.uint8
-E4X4 = mybir.dt.float8_e4m3fn_x4
-E5X4 = mybir.dt.float8_e5m2_x4
+E4M3_X4 = mybir.dt.float8_e4m3fn_x4
+E5M2_X4 = mybir.dt.float8_e5m2_x4
 ACT = mybir.ActivationFunctionType
 ALU = mybir.AluOpType
 
 P = 128
-J = 4
-FW = 512
+PACK = 4
+TOKENS = P * PACK
+HEAD_DIM = 512
+BANK_F32 = 512
 EPS = 1e-5
+
+GPSIMD_COLS = 128
+VECTOR_COLS = HEAD_DIM - GPSIMD_COLS
 
 FLOPS = 2 * 1024 * 512 * 512 * 2 + 6 * 2 * 512 * 512 * 1024
 BYTES = 1024 * 3072 * 4 + 1024 * 3072 * 2 + 3 * 1024 * 1024 * 2 + 2 * 512 * 512 * 2 + 2 * 3072 * 2 + 1024 * 1024 * 4 + 6 * 512 * 512 * 4
 
 
-XI_SPLIT = ((512, 0), (512, 0), (512, 0))
-VI_ON_S = False
-W_ON_S = False
-D_G = 128
-FAST = True
-
-
 def tile_mom_v_kernel(tc, x1, x2, x3, W, b, gamma, beta, running_mean, running_var, y, grad_out, out_0, out_1):
     nc = tc.nc
-    xs = (x1, x2, x3)
-    units = [(e, g, h) for e in range(3) for g in range(2) for h in range(2)]
+    x_of_expert = (x1, x2, x3)
+    units = [(e, i, h) for e in range(3) for i in range(2) for h in range(2)]
     n_units = len(units)
     last = n_units - 1
     w_rows = W.rearrange("h e f d -> (h e f) d")
-    o1_rows = out_1.rearrange("h e f d -> (h e f) d")
+    out_1_rows = out_1.rearrange("h e f d -> (h e f) d")
+    var_rows = running_var.rearrange("h e f -> (h e) f")
+    gamma_rows = gamma.rearrange("h e f -> (h e) f")
+
+    def chunk_of(u):
+        e, i, h = units[u]
+        return 2 * e + h
+
+    def first_unit(chunk):
+        return 4 * (chunk // 2) + chunk % 2
+
+    def row_of_chunk(chunk):
+        return 3 * (chunk % 2) + chunk // 2
+
+    def is_unit(u):
+        return 0 <= u < n_units
+
+    def is_expert0(u):
+        return is_unit(u) and units[u][0] == 0
+
+    def is_later_expert(u):
+        return is_unit(u) and units[u][0] > 0
+
+    def closes_chunk(u):
+        return units[u][1] == 1
+
+    def slot_ranges(u):
+        return [(0, 1), (1, 2), (2, PACK)] if u == 0 else [(0, PACK)]
 
     with ExitStack() as ctx:
         ctx.enter_context(tc.manual_schedule())
-        sb = ctx.enter_context(tc.tile_pool(name="sb", bufs=1))
-        ps = ctx.enter_context(tc.psum_pool(name="ps", bufs=1))
+        sbuf = ctx.enter_context(tc.tile_pool(name="sbuf", bufs=1))
+        psum = ctx.enter_context(tc.psum_pool(name="psum", bufs=1))
 
-        t_y = {}
-        t_g = {}
-        t_x = {}
-        t_p = {}
-        t_xg = {}
-        t_dyn = {}
-        t_dyi = {}
-        t_g0 = {}
-        t_c0 = {}
-        t_dc = {}
-        t_xc = {}
-        t_cb = {}
-        t_cs = {}
-        t_tp = {}
-        t_acc0 = {}
-        t_acc1 = {}
-        t_o1 = {}
-        t_w = {}
+        y_tiles = {}
+        g_tiles = {}
+        x_tiles = {}
+        prod_tiles = {}
+        x_grouped = {}
+        dy_plain = {}
+        dy_grouped = {}
+        dyT_banks = {}
+        dyT_grouped = {}
+        dyT_mx = {}
+        dy_mx = {}
+        x_mx = {}
+        c_banks = {}
+        c_for_gpsimd = {}
+        out_0_banks = {}
+        out_1_banks = {}
+        w_tiles = {}
+        w_grouped = {}
 
-        warm = sb.tile([P, 1], F32, name="warm", tag="warm")
-        warm2 = sb.tile([P, 1], F32, name="warm2", tag="warm2")
-        nc.vector.memset(warm[:], 1.0)
-        nc.scalar.activation(out=warm2[:], in_=warm[:], func=ACT.Sqrt)
-        gam = sb.tile([P, FW], BF16, name="gam", tag="gam")
-        var = sb.tile([P, FW], BF16, name="var", tag="var")
-        nc.vector.memset(var[:], 0.0)
-        nc.vector.memset(gam[:], 0.0)
-        var_rows = running_var.rearrange("h e f -> (h e) f")
-        gam_rows = gamma.rearrange("h e f -> (h e) f")
-        nc.sync.dma_start(out=var[0:4, :], in_=var_rows[0:4, :])
-        nc.sync.dma_start(out=var[4:6, :], in_=var_rows[4:6, :])
-        ident = sb.tile([P, P], F32, name="ident", tag="ident")
-        make_identity(nc, ident[:])
-        sd = sb.tile([P, FW], F32, name="sd", tag="sd")
-        rs = sb.tile([P, FW], F32, name="rs", tag="rs")
-        c3 = sb.tile([P, FW], F32, name="c3", tag="c3")
-        nc.scalar.activation(out=sd[:], in_=var[:], func=ACT.Sqrt, bias=EPS, scale=1.0)
-        nc.scalar.activation(out=warm2[:], in_=warm[:], func=ACT.Tanh)
+        one = sbuf.tile([P, 1], F32, name="one", tag="one")
+        unused = sbuf.tile([P, 1], F32, name="unused", tag="unused")
+        nc.vector.memset(one[:], 1.0)
+        nc.scalar.activation(out=unused[:], in_=one[:], func=ACT.Sqrt)
+        gamma_sb = sbuf.tile([P, HEAD_DIM], BF16, name="gamma_sb", tag="gamma_sb")
+        var_sb = sbuf.tile([P, HEAD_DIM], BF16, name="var_sb", tag="var_sb")
+        nc.vector.memset(var_sb[:], 0.0)
+        nc.vector.memset(gamma_sb[:], 0.0)
+        nc.sync.dma_start(out=var_sb[0:4, :], in_=var_rows[0:4, :])
+        nc.sync.dma_start(out=var_sb[4:6, :], in_=var_rows[4:6, :])
+        identity = sbuf.tile([P, P], F32, name="identity", tag="identity")
+        make_identity(nc, identity[:])
+        std = sbuf.tile([P, HEAD_DIM], F32, name="std", tag="std")
+        inv_std = sbuf.tile([P, HEAD_DIM], F32, name="inv_std", tag="inv_std")
+        c_rows = sbuf.tile([P, HEAD_DIM], F32, name="c_rows", tag="c_rows")
+        nc.scalar.activation(out=std[:], in_=var_sb[:], func=ACT.Sqrt, bias=EPS, scale=1.0)
+        nc.scalar.activation(out=unused[:], in_=one[:], func=ACT.Tanh)
 
-        w_codes = sb.tile([P, 2, FW], U32, name="w_codes", tag="w_codes", align_bytes=64)
-        w_scales = sb.tile([P, 2, FW], U8, name="w_scales", tag="w_scales", align_bytes=64)
+        w_codes = sbuf.tile([P, 2, HEAD_DIM], U32, name="w_codes", tag="w_codes", align_bytes=64)
+        w_scales = sbuf.tile([P, 2, HEAD_DIM], U8, name="w_scales", tag="w_scales", align_bytes=64)
 
-        def interleave(eng, dst, src):
-            if FAST:
-                d = dst.rearrange("p (c i) t -> p c t i", i=4)
-                s_ = src.rearrange("p t (c i) -> p c t i", i=4)
-            else:
-                d = dst
-                s_ = src.rearrange("p t c -> p c t")
-            if eng == "S":
-                nc.scalar.copy(out=d, in_=s_)
-            elif eng == "V":
-                nc.vector.tensor_copy(out=d, in_=s_)
-            else:
-                nc.gpsimd.tensor_scalar(out=d, in0=s_, scalar1=1.0, scalar2=0.0, op0=ALU.mult, op1=ALU.add)
+        def interleaved(grouped, rows):
+            return grouped.rearrange("p (m k) t -> p m t k", k=4), rows.rearrange("p t (m k) -> p m t k", k=4)
 
-        def make_c3():
-            nc.vector.reciprocal(out=rs[:], in_=sd[:])
-            nc.vector.scalar_tensor_tensor(out=c3[:], in0=rs[:], scalar=-0.5, in1=gam[:], op0=ALU.mult, op1=ALU.mult)
+        def make_c_rows():
+            nc.vector.reciprocal(out=inv_std[:], in_=std[:])
+            nc.vector.scalar_tensor_tensor(out=c_rows[:], in0=inv_std[:], scalar=-0.5, in1=gamma_sb[:], op0=ALU.mult, op1=ALU.mult)
 
-        def spread_c(c):
-            e, h = c // 2, c % 2
-            r = 3 * h + e
-            cb = ps.tile([P, FW], F32, name="cb", tag="cb", bufs=2)
-            nc.tensor.matmul(out=cb[:], lhsT=ident[:, r : r + 1].to_broadcast([P, P]), rhs=c3[:], start=True, stop=True)
-            t_cb[c] = cb
+        def spread_c(chunk):
+            r = row_of_chunk(chunk)
+            bank = psum.tile([P, HEAD_DIM], F32, name="c_bank", tag="c_bank", bufs=2)
+            nc.tensor.matmul(out=bank[:], lhsT=identity[:, r : r + 1].to_broadcast([P, P]), rhs=c_rows[:], start=True, stop=True)
+            c_banks[chunk] = bank
 
-        def copy_c(c):
-            cs = sb.tile([P, D_G], F32, name="cb_sb", tag="cb_sb", bufs=3)
-            nc.scalar.copy(out=cs[:], in_=t_cb[c][:, FW - D_G : FW])
-            t_cs[c] = cs
+        def copy_c_for_gpsimd(chunk):
+            c_sb = sbuf.tile([P, GPSIMD_COLS], F32, name="c_for_gpsimd", tag="c_for_gpsimd", bufs=3)
+            nc.scalar.copy(out=c_sb[:], in_=c_banks[chunk][:, VECTOR_COLS:HEAD_DIM])
+            c_for_gpsimd[chunk] = c_sb
 
-        def load(u):
-            e, g, h = units[u]
-            r0 = 512 * g
-            c0 = 512 * (2 * e + h)
-            first = e == 0 and g == 0
-            g_src = grad_out[r0 : r0 + 512, 1024 * e : 1024 * e + 1024].rearrange("(p j) w -> p j w", j=J)
-            y_src = y[r0 : r0 + 512, c0 : c0 + 512].rearrange("(p j) w -> p j w", j=J)
-            hs = slice(512 * h, 512 * h + 512)
+        def load_y_and_g(u):
+            e, i, h = units[u]
+            tokens = slice(TOKENS * i, TOKENS * (i + 1))
+            g_src = grad_out[tokens, 2 * HEAD_DIM * e : 2 * HEAD_DIM * (e + 1)].rearrange("(p j) w -> p j w", j=PACK)
+            y_src = y[tokens, HEAD_DIM * chunk_of(u) : HEAD_DIM * (chunk_of(u) + 1)].rearrange("(p j) w -> p j w", j=PACK)
+            head_cols = slice(HEAD_DIM * h, HEAD_DIM * (h + 1))
             if h == 0:
-                gt = sb.tile([P, J, 2 * FW], BF16, name="g_raw", tag="g_raw", bufs=3)
-                t_g[(e, g)] = gt
-            yt = sb.tile([P, J, FW], F32, name="y_raw", tag="y_raw", bufs=4)
-            t_y[u] = yt
+                g_tiles[(e, i)] = sbuf.tile([P, PACK, 2 * HEAD_DIM], BF16, name="g_sb", tag="g_sb", bufs=3)
+            g_sb = g_tiles[(e, i)]
+            y_sb = sbuf.tile([P, PACK, HEAD_DIM], F32, name="y_sb", tag="y_sb", bufs=4)
+            y_tiles[u] = y_sb
             if u == 0:
-                nc.sync.dma_start(out=yt[:, 0:1, :], in_=y_src[:, 0:1, :])
-                nc.sync.dma_start(out=yt[:, 1:2, :], in_=y_src[:, 1:2, :])
-                nc.sync.dma_start(out=t_g[(e, g)][:, :, hs], in_=g_src[:, :, hs])
-                nc.sync.dma_start(out=yt[:, 2:4, :], in_=y_src[:, 2:4, :])
-                nc.sync.dma_start(out=gam[0:4, :], in_=gam_rows[0:4, :])
-                nc.sync.dma_start(out=gam[4:6, :], in_=gam_rows[4:6, :])
-            elif first:
-                nc.sync.dma_start(out=yt[:], in_=y_src)
-                nc.sync.dma_start(out=t_g[(e, g)][:, :, hs], in_=g_src[:, :, hs])
+                nc.sync.dma_start(out=y_sb[:, 0:1, :], in_=y_src[:, 0:1, :])
+                nc.sync.dma_start(out=y_sb[:, 1:2, :], in_=y_src[:, 1:2, :])
+                nc.sync.dma_start(out=g_sb[:, :, head_cols], in_=g_src[:, :, head_cols])
+                nc.sync.dma_start(out=y_sb[:, 2:4, :], in_=y_src[:, 2:4, :])
+                nc.sync.dma_start(out=gamma_sb[0:4, :], in_=gamma_rows[0:4, :])
+                nc.sync.dma_start(out=gamma_sb[4:6, :], in_=gamma_rows[4:6, :])
+            elif u == 1:
+                nc.sync.dma_start(out=y_sb[:], in_=y_src)
+                nc.sync.dma_start(out=g_sb[:, :, head_cols], in_=g_src[:, :, head_cols])
             else:
                 if h == 0:
-                    nc.sync.dma_start(out=t_g[(e, g)][:], in_=g_src)
-                nc.sync.dma_start(out=yt[:], in_=y_src)
+                    nc.sync.dma_start(out=g_sb[:], in_=g_src)
+                nc.sync.dma_start(out=y_sb[:], in_=y_src)
 
         def load_x(u):
-            e, g, h = units[u]
+            e, i, h = units[u]
             if h == 0:
-                r0 = 512 * g
-                xt = sb.tile([P, J, 2 * FW], BF16, name="x_raw", tag="x_raw", bufs=2)
-                nc.sync.dma_start(out=xt[:], in_=xs[e][r0 : r0 + 512, :].rearrange("(p j) w -> p j w", j=J))
-                t_x[(e, g)] = xt
+                x_sb = sbuf.tile([P, PACK, 2 * HEAD_DIM], BF16, name="x_sb", tag="x_sb", bufs=2)
+                nc.sync.dma_start(out=x_sb[:], in_=x_of_expert[e][TOKENS * i : TOKENS * (i + 1), :].rearrange("(p j) w -> p j w", j=PACK))
+                x_tiles[(e, i)] = x_sb
 
         def load_w(h):
-            wr = sb.tile([P, J, FW], BF16, name="w_raw", tag="w_raw", bufs=2)
-            f0 = 3 * h * 512
-            nc.sync.dma_start(out=wr[:], in_=w_rows[f0 : f0 + 512, :].rearrange("(q t) d -> q t d", t=J))
-            t_w[h] = wr
+            w_sb = sbuf.tile([P, PACK, HEAD_DIM], BF16, name="w_sb", tag="w_sb", bufs=2)
+            f0 = HEAD_DIM * row_of_chunk(h)
+            nc.sync.dma_start(out=w_sb[:], in_=w_rows[f0 : f0 + HEAD_DIM, :].rearrange("(q t) d -> q t d", t=PACK))
+            w_tiles[h] = w_sb
 
-        def w_interleave(h):
-            wg = sb.tile([P, FW, J], BF16, name="w_grp", tag="w_grp", bufs=2, align_bytes=64)
-            interleave("S" if W_ON_S else "V", wg[:], t_w[h][:])
-            t_w[(h, 1)] = wg
+        def interleave_w(h):
+            grouped = sbuf.tile([P, HEAD_DIM, PACK], BF16, name="w_grouped", tag="w_grouped", bufs=2, align_bytes=64)
+            dst, src = interleaved(grouped[:], w_tiles[h][:])
+            nc.vector.tensor_copy(out=dst, in_=src)
+            w_grouped[h] = grouped
 
-        def w_quant(h):
-            nc.vector.quantize_mx(out=w_codes[:, h, :].bitcast(E4X4), scales=w_scales[:, h, :], in_=t_w[(h, 1)][:].rearrange("q d t -> q (d t)"))
+        def quantize_w(h):
+            nc.vector.quantize_mx(out=w_codes[:, h, :].bitcast(E4M3_X4), scales=w_scales[:, h, :], in_=w_grouped[h][:].rearrange("q d t -> q (d t)"))
 
-        def slices(u):
-            return [(0, 1), (1, 2), (2, 4)] if u == 0 else [(0, J)]
+        def tanh_and_silu(u):
+            prod = sbuf.tile([P, PACK, HEAD_DIM], F32, name="prod", tag="prod", bufs=3)
+            y_sb = y_tiles[u]
+            for a, z in slot_ranges(u):
+                nc.scalar.activation(out=prod[:, a:z, :], in_=y_sb[:, a:z, :], func=ACT.Tanh, scale=0.851)
+            for a, z in slot_ranges(u):
+                nc.scalar.activation(out=y_sb[:, a:z, :], in_=y_sb[:, a:z, :], func=ACT.Silu, scale=-1.702)
+            prod_tiles[u] = prod
 
-        def acts(u):
-            pt = sb.tile([P, J, FW], F32, name="p_t", tag="p_t", bufs=3)
-            yt = t_y[u]
-            for a, z in slices(u):
-                nc.scalar.activation(out=pt[:, a:z, :], in_=yt[:, a:z, :], func=ACT.Tanh, scale=0.851)
-            for a, z in slices(u):
-                nc.scalar.activation(out=yt[:, a:z, :], in_=yt[:, a:z, :], func=ACT.Silu, scale=-1.702)
-            t_p[u] = pt
+        def interleave_x(u):
+            e, i, h = units[u]
+            grouped = sbuf.tile([P, HEAD_DIM, PACK], BF16, name="x_grouped", tag="x_grouped", bufs=2, align_bytes=64)
+            x_grouped[u] = grouped
+            dst, src = interleaved(grouped[:], x_tiles[(e, i)][:, :, HEAD_DIM * h : HEAD_DIM * (h + 1)])
+            nc.scalar.copy(out=dst, in_=src)
 
-        def x_alloc(u):
-            xg = sb.tile([P, FW, J], BF16, name="x_grp", tag="x_grp", bufs=2, align_bytes=64)
-            t_xg[u] = xg
-
-        def x_interleave(u, eng):
-            e, g, h = units[u]
-            n_s, n_g = XI_SPLIT[e]
-            lo, hi = {"S": (0, n_s), "G": (n_s, n_s + n_g), "V": (n_s + n_g, FW)}[eng]
-            if hi > lo:
-                interleave(eng, t_xg[u][:, lo:hi, :], t_x[(e, g)][:, :, 512 * h + lo : 512 * h + hi])
-
-        def v_a(u):
-            e, g, h = units[u]
-            pt = t_p[u]
-            for a, z in slices(u):
+        def times_g(u):
+            e, i, h = units[u]
+            prod = prod_tiles[u]
+            for a, z in slot_ranges(u):
                 nc.vector.scalar_tensor_tensor(
-                    out=pt[:, a:z, :], in0=pt[:, a:z, :], scalar=1.0, in1=t_g[(e, g)][:, a:z, 512 * h : 512 * h + 512], op0=ALU.add, op1=ALU.mult
+                    out=prod[:, a:z, :], in0=prod[:, a:z, :], scalar=1.0, in1=g_tiles[(e, i)][:, a:z, HEAD_DIM * h : HEAD_DIM * (h + 1)], op0=ALU.add, op1=ALU.mult
                 )
 
-        def v_b(u):
-            for a, z in slices(u):
+        def times_silu(u):
+            prod = prod_tiles[u]
+            for a, z in slot_ranges(u):
                 nc.vector.scalar_tensor_tensor(
-                    out=t_p[u][:, a:z, :], in0=t_y[u][:, a:z, :], scalar=1.0, in1=t_p[u][:, a:z, :], op0=ALU.subtract, op1=ALU.mult
+                    out=prod[:, a:z, :], in0=y_tiles[u][:, a:z, :], scalar=1.0, in1=prod[:, a:z, :], op0=ALU.subtract, op1=ALU.mult
                 )
 
-        def d_alloc(u):
-            dyi = sb.tile([P, FW, J], BF16, name="dyi", tag="dyi", bufs=3, align_bytes=64)
-            t_dyi[u] = dyi
+        def new_dy_grouped(u):
+            dy_grouped[u] = sbuf.tile([P, HEAD_DIM, PACK], BF16, name="dy_grouped", tag="dy_grouped", bufs=3, align_bytes=64)
 
-        def d_pass(eng, u, lo, hi, cvals):
+        def new_dy_plain(u):
+            dy_plain[u] = sbuf.tile([P, PACK, HEAD_DIM], BF16, name="dy_plain", tag="dy_plain", bufs=2)
+
+        def times_c(engine, u, lo, hi, c_values):
             if units[u][0] == 0:
-                eng.tensor_tensor(
-                    out=t_dyn[u][:, :, lo:hi], in0=t_p[u][:, :, lo:hi], in1=cvals.unsqueeze(1).to_broadcast([P, J, hi - lo]), op=ALU.mult
+                engine.tensor_tensor(
+                    out=dy_plain[u][:, :, lo:hi], in0=prod_tiles[u][:, :, lo:hi], in1=c_values.unsqueeze(1).to_broadcast([P, PACK, hi - lo]), op=ALU.mult
                 )
             else:
-                eng.tensor_tensor(
-                    out=t_dyi[u][:, lo:hi, :],
-                    in0=t_p[u][:, :, lo:hi].rearrange("p j f -> p f j"),
-                    in1=cvals.unsqueeze(2).to_broadcast([P, hi - lo, J]),
+                engine.tensor_tensor(
+                    out=dy_grouped[u][:, lo:hi, :],
+                    in0=prod_tiles[u][:, :, lo:hi].rearrange("p j f -> p f j"),
+                    in1=c_values.unsqueeze(2).to_broadcast([P, hi - lo, PACK]),
                     op=ALU.mult,
                 )
 
-        def v_d(u, lo=0, hi=FW):
-            e, g, h = units[u]
-            d_pass(nc.vector, u, lo, hi, t_cb[2 * e + h][:, lo:hi])
+        def times_c_on_vector(u, lo, hi):
+            times_c(nc.vector, u, lo, hi, c_banks[chunk_of(u)][:, lo:hi])
 
-        def g_d(u):
-            e, g, h = units[u]
-            d_pass(nc.gpsimd, u, FW - D_G, FW, t_cs[2 * e + h][:])
+        def times_c_on_gpsimd(u):
+            times_c(nc.gpsimd, u, VECTOR_COLS, HEAD_DIM, c_for_gpsimd[chunk_of(u)][:])
 
-        def dyn_alloc(u):
-            dyn = sb.tile([P, J, FW], BF16, name="dyn", tag="dyn", bufs=2)
-            t_dyn[u] = dyn
+        def interleave_dy(u):
+            new_dy_grouped(u)
+            dst, src = interleaved(dy_grouped[u][:], dy_plain[u][:])
+            nc.vector.tensor_copy(out=dst, in_=src)
 
-        def v_i(u):
-            d_alloc(u)
-            interleave("S" if VI_ON_S else "V", t_dyi[u][:], t_dyn[u][:])
+        def quantize_dy(u, lo=0, hi=HEAD_DIM):
+            i = units[u][1]
+            chunk = chunk_of(u)
+            if i == 0:
+                codes = sbuf.tile([P, 2, HEAD_DIM], U32, name="dy_codes", tag="dy_codes", bufs=3, align_bytes=64)
+                scales = sbuf.tile([P, 2, HEAD_DIM], U8, name="dy_scales", tag="dy_scales", bufs=3, align_bytes=64)
+                dy_mx[chunk] = (codes, scales)
+            codes, scales = dy_mx[chunk]
+            nc.vector.quantize_mx(
+                out=codes[:, i, lo:hi].bitcast(E5M2_X4), scales=scales[:, i, lo:hi], in_=dy_grouped[u][:, lo:hi, :].rearrange("p f j -> p (f j)")
+            )
 
-        def q_d(u, lo=0, hi=FW):
-            e, g, h = units[u]
-            c = 2 * e + h
-            if g == 0:
-                dc = sb.tile([P, 2, FW], U32, name="d_codes", tag="d_codes", bufs=3, align_bytes=64)
-                ds = sb.tile([P, 2, FW], U8, name="d_scales", tag="d_scales", bufs=3, align_bytes=64)
-                t_dc[c] = (dc, ds)
-            dc, ds = t_dc[c]
-            nc.vector.quantize_mx(out=dc[:, g, lo:hi].bitcast(E5X4), scales=ds[:, g, lo:hi], in_=t_dyi[u][:, lo:hi, :].rearrange("p f j -> p (f j)"))
+        def quantize_x(u):
+            i = units[u][1]
+            chunk = chunk_of(u)
+            if i == 0:
+                codes = sbuf.tile([P, 2, HEAD_DIM], U32, name="x_codes", tag="x_codes", bufs=4, align_bytes=64)
+                scales = sbuf.tile([P, 2, HEAD_DIM], U8, name="x_scales", tag="x_scales", bufs=4, align_bytes=64)
+                x_mx[chunk] = (codes, scales)
+            codes, scales = x_mx[chunk]
+            nc.vector.quantize_mx(out=codes[:, i, :].bitcast(E4M3_X4), scales=scales[:, i, :], in_=x_grouped[u][:].rearrange("p w j -> p (w j)"))
 
-        def q_x(u):
-            e, g, h = units[u]
-            c = 2 * e + h
-            if g == 0:
-                xc = sb.tile([P, 2, FW], U32, name="x_codes", tag="x_codes", bufs=4, align_bytes=64)
-                xsc = sb.tile([P, 2, FW], U8, name="x_scales", tag="x_scales", bufs=4, align_bytes=64)
-                t_xc[c] = (xc, xsc)
-            xc, xsc = t_xc[c]
-            nc.vector.quantize_mx(out=xc[:, g, :].bitcast(E4X4), scales=xsc[:, g, :], in_=t_xg[u][:].rearrange("p w j -> p (w j)"))
+        def new_bank(name):
+            return psum.tile([P, BANK_F32], F32, name=name, tag="bank", bufs=6)
 
-        def t_0(u):
-            words = t_dyn[u][:].rearrange("p j f -> p (j f)").bitcast(F32)
+        def transpose_dy(u):
+            words = dy_plain[u][:].rearrange("p j f -> p (j f)").bitcast(F32)
+            words_of_slot = HEAD_DIM // 2
             banks = []
-            for jp in range(2):
-                tp = ps.tile([P, FW], F32, name="tp", tag="bank", bufs=6)
-                tpv = tp[:].rearrange("q (a v r) -> q a v r", a=2, v=2)
+            for slot_pair in range(2):
+                bank = new_bank("dyT_bank")
+                by_slot = bank[:].rearrange("q (a v p) -> q a v p", a=2, v=2)
                 for a in range(2):
-                    j = 2 * jp + a
+                    j = 2 * slot_pair + a
                     for v in range(2):
-                        nc.tensor.transpose(tpv[:, a, v, :], words[:, 256 * j + v : 256 * (j + 1) : 2], ident[:])
-                banks.append(tp)
-            t_tp[u] = banks
+                        nc.tensor.transpose(by_slot[:, a, v, :], words[:, words_of_slot * j + v : words_of_slot * (j + 1) : 2], identity[:])
+                banks.append(bank)
+            dyT_banks[u] = banks
 
-        def c_0(u):
-            g0 = sb.tile([P, FW, J], BF16, name="g0", tag="g0", bufs=2, align_bytes=64)
-            g0w = g0[:].rearrange("q c t -> q (c t)").bitcast(F32).rearrange("q (a r v) -> q a r v", a=4, v=2)
-            for jp in range(2):
-                tpv = t_tp[u][jp][:].rearrange("q (a v r) -> q a r v", a=2, v=2)
-                nc.scalar.copy(out=g0w[:, 2 * jp : 2 * jp + 2, :, :], in_=tpv)
-            t_g0[u] = g0
+        def copy_dyT(u):
+            grouped = sbuf.tile([P, TOKENS, PACK], BF16, name="dyT_grouped", tag="dyT_grouped", bufs=2, align_bytes=64)
+            words = grouped[:].rearrange("q n t -> q (n t)").bitcast(F32).rearrange("q (j p v) -> q j p v", j=PACK, v=2)
+            for slot_pair in range(2):
+                nc.scalar.copy(out=words[:, 2 * slot_pair : 2 * slot_pair + 2, :, :], in_=dyT_banks[u][slot_pair][:].rearrange("q (a v p) -> q a p v", a=2, v=2))
+            dyT_grouped[u] = grouped
 
-        def q_0(u):
-            c0 = sb.tile([P, FW], U32, name="c0", tag="c0", bufs=2, align_bytes=64)
-            s0 = sb.tile([P, FW], U8, name="s0", tag="s0", bufs=2, align_bytes=64)
-            nc.vector.quantize_mx(out=c0[:].bitcast(E5X4), scales=s0[:], in_=t_g0[u][:].rearrange("q c t -> q (c t)"))
-            t_c0[u] = (c0, s0)
+        def quantize_dyT(u):
+            codes = sbuf.tile([P, TOKENS], U32, name="dyT_codes", tag="dyT_codes", bufs=2, align_bytes=64)
+            scales = sbuf.tile([P, TOKENS], U8, name="dyT_scales", tag="dyT_scales", bufs=2, align_bytes=64)
+            nc.vector.quantize_mx(out=codes[:].bitcast(E5M2_X4), scales=scales[:], in_=dyT_grouped[u][:].rearrange("q n t -> q (n t)"))
+            dyT_mx[u] = (codes, scales)
 
-        def m_0(u):
-            e, g, h = units[u]
-            c0, s0 = t_c0[u]
+        def multiply_out_0(u):
+            h = units[u][2]
+            codes, scales = dyT_mx[u]
             banks = []
-            for j in range(J):
-                acc = ps.tile([P, FW], F32, name="acc0", tag="bank", bufs=6)
+            for j in range(PACK):
+                bank = new_bank("out_0_bank")
                 nc.tensor.matmul_mx(
-                    out=acc[:],
-                    lhsT=c0[:, 128 * j : 128 * j + 128].bitcast(E5X4),
-                    lhsT_scale=s0[:, 128 * j : 128 * j + 128],
-                    rhs=w_codes[:, h, :].bitcast(E4X4),
+                    out=bank[:],
+                    lhsT=codes[:, P * j : P * (j + 1)].bitcast(E5M2_X4),
+                    lhsT_scale=scales[:, P * j : P * (j + 1)],
+                    rhs=w_codes[:, h, :].bitcast(E4M3_X4),
                     rhs_scale=w_scales[:, h, :],
                     start=True,
                     stop=True,
                 )
-                banks.append(acc)
-            t_acc0[u] = banks
+                banks.append(bank)
+            out_0_banks[u] = banks
 
-        def e_0(u):
-            e, g, h = units[u]
-            o0 = sb.tile([P, J, FW], F32, name="o0", tag="ost", bufs=2)
-            for j in range(J):
-                nc.scalar.copy(out=o0[:, j, :], in_=t_acc0[u][j][:])
-            nc.sync.dma_start(out=out_0[512 * g : 512 * g + 512, 512 * h : 512 * h + 512].rearrange("(p j) d -> p j d", j=J), in_=o0[:])
+        def new_staging(name):
+            return sbuf.tile([P, 4, BANK_F32], F32, name=name, tag="staging", bufs=2)
 
-        def m_1(c, ft):
-            dc, ds = t_dc[c]
-            xc, xsc = t_xc[c]
-            acc = ps.tile([P, FW], F32, name="acc1", tag="bank", bufs=6)
-            for g in range(2):
+        def store_out_0(u):
+            e, i, h = units[u]
+            staging = new_staging("out_0_staging")
+            for j in range(PACK):
+                nc.scalar.copy(out=staging[:, j, :], in_=out_0_banks[u][j][:])
+            nc.sync.dma_start(
+                out=out_0[TOKENS * i : TOKENS * (i + 1), HEAD_DIM * h : HEAD_DIM * (h + 1)].rearrange("(p j) d -> p j d", j=PACK), in_=staging[:]
+            )
+
+        def multiply_out_1(chunk, f_tile):
+            dy_codes, dy_scales = dy_mx[chunk]
+            x_codes, x_scales = x_mx[chunk]
+            bank = new_bank("out_1_bank")
+            for i in range(2):
                 nc.tensor.matmul_mx(
-                    out=acc[:],
-                    lhsT=dc[:, g, 128 * ft : 128 * ft + 128].bitcast(E5X4),
-                    lhsT_scale=ds[:, g, 128 * ft : 128 * ft + 128],
-                    rhs=xc[:, g, :].bitcast(E4X4),
-                    rhs_scale=xsc[:, g, :],
-                    start=(g == 0),
-                    stop=(g == 1),
+                    out=bank[:],
+                    lhsT=dy_codes[:, i, P * f_tile : P * (f_tile + 1)].bitcast(E5M2_X4),
+                    lhsT_scale=dy_scales[:, i, P * f_tile : P * (f_tile + 1)],
+                    rhs=x_codes[:, i, :].bitcast(E4M3_X4),
+                    rhs_scale=x_scales[:, i, :],
+                    start=(i == 0),
+                    stop=(i == 1),
                 )
-            t_acc1[(c, ft)] = acc
+            out_1_banks[(chunk, f_tile)] = bank
 
-        def o1_dst(c):
-            f0 = (3 * (c % 2) + c // 2) * 512
-            return o1_rows[f0 : f0 + 512, :].rearrange("(t p) d -> p t d", p=P)
+        def out_1_of_chunk(chunk):
+            f0 = HEAD_DIM * row_of_chunk(chunk)
+            return out_1_rows[f0 : f0 + HEAD_DIM, :].rearrange("(t p) d -> p t d", p=P)
 
-        def e_1(c):
-            o1 = sb.tile([P, 4, FW], F32, name="o1", tag="ost", bufs=2)
-            for ft in range(4):
-                nc.scalar.copy(out=o1[:, ft, :], in_=t_acc1[(c, ft)][:])
-            nc.sync.dma_start(out=o1_dst(c), in_=o1[:])
+        def store_out_1(chunk):
+            staging = new_staging("out_1_staging")
+            for f_tile in range(4):
+                nc.scalar.copy(out=staging[:, f_tile, :], in_=out_1_banks[(chunk, f_tile)][:])
+            nc.sync.dma_start(out=out_1_of_chunk(chunk), in_=staging[:])
 
-        def e_1_tail(c, ft):
-            if ft == 0:
-                t_o1[c] = sb.tile([P, 4, FW], F32, name="o1", tag="ost", bufs=2)
-            o1 = t_o1[c]
-            if ft % 2 == 0:
-                nc.scalar.copy(out=o1[:, ft, :], in_=t_acc1[(c, ft)][:])
-            else:
-                nc.vector.tensor_copy(out=o1[:, ft, :], in_=t_acc1[(c, ft)][:])
-            nc.sync.dma_start(out=o1_dst(c)[:, ft : ft + 1, :], in_=o1[:, ft : ft + 1, :])
+        def finish_last_unit(u):
+            chunk = chunk_of(u)
+            quantize_x(u)
+            new_dy_grouped(u)
+            for k in range(4):
+                times_c_on_vector(u, P * k, P * (k + 1))
+                if k > 0:
+                    quantize_dy(u, P * (k - 1), P * k)
+                    multiply_out_1(chunk, k - 1)
+            quantize_dy(u, P * 3, P * 4)
+            multiply_out_1(chunk, 3)
+            staging = new_staging("out_1_staging")
+            for f_tile in range(4):
+                if f_tile % 2 == 0:
+                    nc.scalar.copy(out=staging[:, f_tile, :], in_=out_1_banks[(chunk, f_tile)][:])
+                else:
+                    nc.vector.tensor_copy(out=staging[:, f_tile, :], in_=out_1_banks[(chunk, f_tile)][:])
+                nc.sync.dma_start(out=out_1_of_chunk(chunk)[:, f_tile : f_tile + 1, :], in_=staging[:, f_tile : f_tile + 1, :])
 
-        def is_unit(u):
-            return 0 <= u < n_units
-
-        def expert0(u):
-            return is_unit(u) and units[u][0] == 0
-
-        def later(u):
-            return is_unit(u) and units[u][0] > 0
-
-        def chunk_done(u):
-            return 2 * units[u][0] + units[u][2] if units[u][1] == 1 else None
-
-        pending_e1 = []
-        for s in range(-3, n_units + 4):
+        unstored_chunks = []
+        for s in range(-3, n_units):
             if is_unit(s + 3):
-                load(s + 3)
+                load_y_and_g(s + 3)
             if is_unit(s + 2):
                 load_x(s + 2)
             if s == 0:
                 load_w(0)
                 load_w(1)
+
+            new_chunks = [chunk for chunk in range(2, 6) if s == first_unit(chunk) - 1]
             if is_unit(s + 1):
-                acts(s + 1)
-            for c in range(2, 6):
-                if s == 4 * (c // 2) + (c % 2) - 1:
-                    spread_c(c)
-            if is_unit(s + 0):
-                x_alloc(s + 0)
-                x_interleave(s + 0, "G")
-                x_interleave(s + 0, "S")
-            for c in range(2, 6):
-                if D_G and s == 4 * (c // 2) + (c % 2) - 1:
-                    copy_c(c)
-            if W_ON_S and s in (1, 2):
-                w_interleave(s - 1)
-            if VI_ON_S and expert0(s - 1):
-                v_i(s - 1)
-            for c in pending_e1:
-                e_1(c)
-            pending_e1 = []
-            if expert0(s - 1):
-                c_0(s - 1)
-            if expert0(s - 3):
-                e_0(s - 3)
+                tanh_and_silu(s + 1)
+            for chunk in new_chunks:
+                spread_c(chunk)
+            if is_unit(s):
+                interleave_x(s)
+            for chunk in new_chunks:
+                copy_c_for_gpsimd(chunk)
+            for chunk in unstored_chunks:
+                store_out_1(chunk)
+            unstored_chunks = []
+            if is_expert0(s - 1):
+                copy_dyT(s - 1)
+            if is_expert0(s - 3):
+                store_out_0(s - 3)
 
             if is_unit(s):
-                v_a(s)
+                times_g(s)
             if s == 0:
-                make_c3()
-                spread_c(0)
-                spread_c(1)
-                if D_G:
-                    copy_c(0)
-                    copy_c(1)
-            if expert0(s - 2):
-                q_d(s - 2)
-            if later(s - 1) and s - 1 != last:
-                q_d(s - 1)
-            done = []
-            if expert0(s - 2) and chunk_done(s - 2) is not None:
-                done.append(chunk_done(s - 2))
-            if later(s - 1) and s - 1 != last and chunk_done(s - 1) is not None:
-                done.append(chunk_done(s - 1))
-            if is_unit(s + 0):
-                x_interleave(s + 0, "V")
+                make_c_rows()
+                for chunk in range(2):
+                    spread_c(chunk)
+                for chunk in range(2):
+                    copy_c_for_gpsimd(chunk)
+            quantised = []
+            if is_expert0(s - 2):
+                quantised.append(s - 2)
+            if is_later_expert(s - 1):
+                quantised.append(s - 1)
+            for u in quantised:
+                quantize_dy(u)
             if is_unit(s - 1):
-                q_x(s - 1)
-            for c in done:
-                for ft in range(4):
-                    m_1(c, ft)
-                pending_e1.append(c)
+                quantize_x(s - 1)
+            for u in quantised:
+                if closes_chunk(u):
+                    for f_tile in range(4):
+                        multiply_out_1(chunk_of(u), f_tile)
+                    unstored_chunks.append(chunk_of(u))
             if is_unit(s):
-                v_b(s)
+                times_silu(s)
             if s == last:
-                for c in pending_e1:
-                    e_1(c)
-                pending_e1 = []
-                q_x(s)
-                d_alloc(s)
-                for k in range(4):
-                    v_d(s, 128 * k, 128 * k + 128)
-                    if k > 0:
-                        q_d(s, 128 * (k - 1), 128 * k)
-                        m_1(5, k - 1)
-                q_d(s, 384, 512)
-                m_1(5, 3)
-                for ft in range(4):
-                    e_1_tail(5, ft)
+                for chunk in unstored_chunks:
+                    store_out_1(chunk)
+                unstored_chunks = []
+                finish_last_unit(s)
             elif is_unit(s):
-                if later(s):
-                    d_alloc(s)
+                if is_expert0(s):
+                    new_dy_plain(s)
                 else:
-                    dyn_alloc(s)
-                if D_G:
-                    g_d(s)
-                v_d(s, 0, FW - D_G)
-                if expert0(s):
-                    t_0(s)
-            if (not W_ON_S) and s in (1, 2):
-                w_interleave(s - 1)
-            if (not VI_ON_S) and expert0(s - 1):
-                v_i(s - 1)
+                    new_dy_grouped(s)
+                times_c_on_gpsimd(s)
+                times_c_on_vector(s, 0, VECTOR_COLS)
+                if is_expert0(s):
+                    transpose_dy(s)
+            if s in (1, 2):
+                interleave_w(s - 1)
+            if is_expert0(s - 1):
+                interleave_dy(s - 1)
             if s in (2, 3):
-                w_quant(s - 2)
-            if expert0(s - 2):
-                q_0(s - 2)
-                m_0(s - 2)
+                quantize_w(s - 2)
+            if is_expert0(s - 2):
+                quantize_dyT(s - 2)
+                multiply_out_0(s - 2)

from contextlib import ExitStack

import concourse.mybir as mybir
from concourse.masks import make_identity

F32 = mybir.dt.float32
BF16 = mybir.dt.bfloat16
U32 = mybir.dt.uint32
U8 = mybir.dt.uint8
E4M3_X4 = mybir.dt.float8_e4m3fn_x4
E5M2_X4 = mybir.dt.float8_e5m2_x4
ACT = mybir.ActivationFunctionType
ALU = mybir.AluOpType

P = 128
PACK = 4
TOKENS = P * PACK
HEAD_DIM = 512
BANK_F32 = 512
EPS = 1e-5

GPSIMD_COLS = 128
VECTOR_COLS = HEAD_DIM - GPSIMD_COLS

FLOPS = 2 * 1024 * 512 * 512 * 2 + 6 * 2 * 512 * 512 * 1024
BYTES = 1024 * 3072 * 4 + 1024 * 3072 * 2 + 3 * 1024 * 1024 * 2 + 2 * 512 * 512 * 2 + 2 * 3072 * 2 + 1024 * 1024 * 4 + 6 * 512 * 512 * 4


def tile_mom_v_kernel(tc, x1, x2, x3, W, b, gamma, beta, running_mean, running_var, y, grad_out, out_0, out_1):
    nc = tc.nc
    x_of_expert = (x1, x2, x3)
    units = [(e, i, h) for e in range(3) for i in range(2) for h in range(2)]
    n_units = len(units)
    last = n_units - 1
    w_rows = W.rearrange("h e f d -> (h e f) d")
    out_1_rows = out_1.rearrange("h e f d -> (h e f) d")
    var_rows = running_var.rearrange("h e f -> (h e) f")
    gamma_rows = gamma.rearrange("h e f -> (h e) f")

    def chunk_of(u):
        e, i, h = units[u]
        return 2 * e + h

    def first_unit(chunk):
        return 4 * (chunk // 2) + chunk % 2

    def row_of_chunk(chunk):
        return 3 * (chunk % 2) + chunk // 2

    def is_unit(u):
        return 0 <= u < n_units

    def is_expert0(u):
        return is_unit(u) and units[u][0] == 0

    def is_later_expert(u):
        return is_unit(u) and units[u][0] > 0

    def closes_chunk(u):
        return units[u][1] == 1

    def slot_ranges(u):
        return [(0, 1), (1, 2), (2, PACK)] if u == 0 else [(0, PACK)]

    with ExitStack() as ctx:
        ctx.enter_context(tc.manual_schedule())
        sbuf = ctx.enter_context(tc.tile_pool(name="sbuf", bufs=1))
        psum = ctx.enter_context(tc.psum_pool(name="psum", bufs=1))

        y_tiles = {}
        g_tiles = {}
        x_tiles = {}
        prod_tiles = {}
        x_grouped = {}
        dy_plain = {}
        dy_grouped = {}
        dyT_banks = {}
        dyT_grouped = {}
        dyT_mx = {}
        dy_mx = {}
        x_mx = {}
        c_banks = {}
        c_for_gpsimd = {}
        out_0_banks = {}
        out_1_banks = {}
        w_tiles = {}
        w_grouped = {}

        one = sbuf.tile([P, 1], F32, name="one", tag="one")
        unused = sbuf.tile([P, 1], F32, name="unused", tag="unused")
        nc.vector.memset(one[:], 1.0)
        nc.scalar.activation(out=unused[:], in_=one[:], func=ACT.Sqrt)
        gamma_sb = sbuf.tile([P, HEAD_DIM], BF16, name="gamma_sb", tag="gamma_sb")
        var_sb = sbuf.tile([P, HEAD_DIM], BF16, name="var_sb", tag="var_sb")
        nc.vector.memset(var_sb[:], 0.0)
        nc.vector.memset(gamma_sb[:], 0.0)
        nc.sync.dma_start(out=var_sb[0:4, :], in_=var_rows[0:4, :])
        nc.sync.dma_start(out=var_sb[4:6, :], in_=var_rows[4:6, :])
        identity = sbuf.tile([P, P], F32, name="identity", tag="identity")
        make_identity(nc, identity[:])
        std = sbuf.tile([P, HEAD_DIM], F32, name="std", tag="std")
        inv_std = sbuf.tile([P, HEAD_DIM], F32, name="inv_std", tag="inv_std")
        c_rows = sbuf.tile([P, HEAD_DIM], F32, name="c_rows", tag="c_rows")
        nc.scalar.activation(out=std[:], in_=var_sb[:], func=ACT.Sqrt, bias=EPS, scale=1.0)
        nc.scalar.activation(out=unused[:], in_=one[:], func=ACT.Tanh)

        w_codes = sbuf.tile([P, 2, HEAD_DIM], U32, name="w_codes", tag="w_codes", align_bytes=64)
        w_scales = sbuf.tile([P, 2, HEAD_DIM], U8, name="w_scales", tag="w_scales", align_bytes=64)

        def interleaved(grouped, rows):
            return grouped.rearrange("p (m k) t -> p m t k", k=4), rows.rearrange("p t (m k) -> p m t k", k=4)

        def make_c_rows():
            nc.vector.reciprocal(out=inv_std[:], in_=std[:])
            nc.vector.scalar_tensor_tensor(out=c_rows[:], in0=inv_std[:], scalar=-0.5, in1=gamma_sb[:], op0=ALU.mult, op1=ALU.mult)

        def spread_c(chunk):
            r = row_of_chunk(chunk)
            bank = psum.tile([P, HEAD_DIM], F32, name="c_bank", tag="c_bank", bufs=2)
            nc.tensor.matmul(out=bank[:], lhsT=identity[:, r : r + 1].to_broadcast([P, P]), rhs=c_rows[:], start=True, stop=True)
            c_banks[chunk] = bank

        def copy_c_for_gpsimd(chunk):
            c_sb = sbuf.tile([P, GPSIMD_COLS], F32, name="c_for_gpsimd", tag="c_for_gpsimd", bufs=3)
            nc.scalar.copy(out=c_sb[:], in_=c_banks[chunk][:, VECTOR_COLS:HEAD_DIM])
            c_for_gpsimd[chunk] = c_sb

        def load_y_and_g(u):
            e, i, h = units[u]
            tokens = slice(TOKENS * i, TOKENS * (i + 1))
            g_src = grad_out[tokens, 2 * HEAD_DIM * e : 2 * HEAD_DIM * (e + 1)].rearrange("(p j) w -> p j w", j=PACK)
            y_src = y[tokens, HEAD_DIM * chunk_of(u) : HEAD_DIM * (chunk_of(u) + 1)].rearrange("(p j) w -> p j w", j=PACK)
            head_cols = slice(HEAD_DIM * h, HEAD_DIM * (h + 1))
            if h == 0:
                g_tiles[(e, i)] = sbuf.tile([P, PACK, 2 * HEAD_DIM], BF16, name="g_sb", tag="g_sb", bufs=3)
            g_sb = g_tiles[(e, i)]
            y_sb = sbuf.tile([P, PACK, HEAD_DIM], F32, name="y_sb", tag="y_sb", bufs=4)
            y_tiles[u] = y_sb
            if u == 0:
                nc.sync.dma_start(out=y_sb[:, 0:1, :], in_=y_src[:, 0:1, :])
                nc.sync.dma_start(out=y_sb[:, 1:2, :], in_=y_src[:, 1:2, :])
                nc.sync.dma_start(out=g_sb[:, :, head_cols], in_=g_src[:, :, head_cols])
                nc.sync.dma_start(out=y_sb[:, 2:4, :], in_=y_src[:, 2:4, :])
                nc.sync.dma_start(out=gamma_sb[0:4, :], in_=gamma_rows[0:4, :])
                nc.sync.dma_start(out=gamma_sb[4:6, :], in_=gamma_rows[4:6, :])
            elif u == 1:
                nc.sync.dma_start(out=y_sb[:], in_=y_src)
                nc.sync.dma_start(out=g_sb[:, :, head_cols], in_=g_src[:, :, head_cols])
            else:
                if h == 0:
                    nc.sync.dma_start(out=g_sb[:], in_=g_src)
                nc.sync.dma_start(out=y_sb[:], in_=y_src)

        def load_x(u):
            e, i, h = units[u]
            if h == 0:
                x_sb = sbuf.tile([P, PACK, 2 * HEAD_DIM], BF16, name="x_sb", tag="x_sb", bufs=2)
                nc.sync.dma_start(out=x_sb[:], in_=x_of_expert[e][TOKENS * i : TOKENS * (i + 1), :].rearrange("(p j) w -> p j w", j=PACK))
                x_tiles[(e, i)] = x_sb

        def load_w(h):
            w_sb = sbuf.tile([P, PACK, HEAD_DIM], BF16, name="w_sb", tag="w_sb", bufs=2)
            f0 = HEAD_DIM * row_of_chunk(h)
            nc.sync.dma_start(out=w_sb[:], in_=w_rows[f0 : f0 + HEAD_DIM, :].rearrange("(q t) d -> q t d", t=PACK))
            w_tiles[h] = w_sb

        def interleave_w(h):
            grouped = sbuf.tile([P, HEAD_DIM, PACK], BF16, name="w_grouped", tag="w_grouped", bufs=2, align_bytes=64)
            dst, src = interleaved(grouped[:], w_tiles[h][:])
            nc.vector.tensor_copy(out=dst, in_=src)
            w_grouped[h] = grouped

        def quantize_w(h):
            nc.vector.quantize_mx(out=w_codes[:, h, :].bitcast(E4M3_X4), scales=w_scales[:, h, :], in_=w_grouped[h][:].rearrange("q d t -> q (d t)"))

        def tanh_and_silu(u):
            prod = sbuf.tile([P, PACK, HEAD_DIM], F32, name="prod", tag="prod", bufs=3)
            y_sb = y_tiles[u]
            for a, z in slot_ranges(u):
                nc.scalar.activation(out=prod[:, a:z, :], in_=y_sb[:, a:z, :], func=ACT.Tanh, scale=0.851)
            for a, z in slot_ranges(u):
                nc.scalar.activation(out=y_sb[:, a:z, :], in_=y_sb[:, a:z, :], func=ACT.Silu, scale=-1.702)
            prod_tiles[u] = prod

        def interleave_x(u):
            e, i, h = units[u]
            grouped = sbuf.tile([P, HEAD_DIM, PACK], BF16, name="x_grouped", tag="x_grouped", bufs=2, align_bytes=64)
            x_grouped[u] = grouped
            dst, src = interleaved(grouped[:], x_tiles[(e, i)][:, :, HEAD_DIM * h : HEAD_DIM * (h + 1)])
            nc.scalar.copy(out=dst, in_=src)

        def times_g(u):
            e, i, h = units[u]
            prod = prod_tiles[u]
            for a, z in slot_ranges(u):
                nc.vector.scalar_tensor_tensor(
                    out=prod[:, a:z, :], in0=prod[:, a:z, :], scalar=1.0, in1=g_tiles[(e, i)][:, a:z, HEAD_DIM * h : HEAD_DIM * (h + 1)], op0=ALU.add, op1=ALU.mult
                )

        def times_silu(u):
            prod = prod_tiles[u]
            for a, z in slot_ranges(u):
                nc.vector.scalar_tensor_tensor(
                    out=prod[:, a:z, :], in0=y_tiles[u][:, a:z, :], scalar=1.0, in1=prod[:, a:z, :], op0=ALU.subtract, op1=ALU.mult
                )

        def new_dy_grouped(u):
            dy_grouped[u] = sbuf.tile([P, HEAD_DIM, PACK], BF16, name="dy_grouped", tag="dy_grouped", bufs=3, align_bytes=64)

        def new_dy_plain(u):
            dy_plain[u] = sbuf.tile([P, PACK, HEAD_DIM], BF16, name="dy_plain", tag="dy_plain", bufs=2)

        def times_c(engine, u, lo, hi, c_values):
            if units[u][0] == 0:
                engine.tensor_tensor(
                    out=dy_plain[u][:, :, lo:hi], in0=prod_tiles[u][:, :, lo:hi], in1=c_values.unsqueeze(1).to_broadcast([P, PACK, hi - lo]), op=ALU.mult
                )
            else:
                engine.tensor_tensor(
                    out=dy_grouped[u][:, lo:hi, :],
                    in0=prod_tiles[u][:, :, lo:hi].rearrange("p j f -> p f j"),
                    in1=c_values.unsqueeze(2).to_broadcast([P, hi - lo, PACK]),
                    op=ALU.mult,
                )

        def times_c_on_vector(u, lo, hi):
            times_c(nc.vector, u, lo, hi, c_banks[chunk_of(u)][:, lo:hi])

        def times_c_on_gpsimd(u):
            times_c(nc.gpsimd, u, VECTOR_COLS, HEAD_DIM, c_for_gpsimd[chunk_of(u)][:])

        def interleave_dy(u):
            new_dy_grouped(u)
            dst, src = interleaved(dy_grouped[u][:], dy_plain[u][:])
            nc.vector.tensor_copy(out=dst, in_=src)

        def quantize_dy(u, lo=0, hi=HEAD_DIM):
            i = units[u][1]
            chunk = chunk_of(u)
            if i == 0:
                codes = sbuf.tile([P, 2, HEAD_DIM], U32, name="dy_codes", tag="dy_codes", bufs=3, align_bytes=64)
                scales = sbuf.tile([P, 2, HEAD_DIM], U8, name="dy_scales", tag="dy_scales", bufs=3, align_bytes=64)
                dy_mx[chunk] = (codes, scales)
            codes, scales = dy_mx[chunk]
            nc.vector.quantize_mx(
                out=codes[:, i, lo:hi].bitcast(E5M2_X4), scales=scales[:, i, lo:hi], in_=dy_grouped[u][:, lo:hi, :].rearrange("p f j -> p (f j)")
            )

        def quantize_x(u):
            i = units[u][1]
            chunk = chunk_of(u)
            if i == 0:
                codes = sbuf.tile([P, 2, HEAD_DIM], U32, name="x_codes", tag="x_codes", bufs=4, align_bytes=64)
                scales = sbuf.tile([P, 2, HEAD_DIM], U8, name="x_scales", tag="x_scales", bufs=4, align_bytes=64)
                x_mx[chunk] = (codes, scales)
            codes, scales = x_mx[chunk]
            nc.vector.quantize_mx(out=codes[:, i, :].bitcast(E4M3_X4), scales=scales[:, i, :], in_=x_grouped[u][:].rearrange("p w j -> p (w j)"))

        def new_bank(name):
            return psum.tile([P, BANK_F32], F32, name=name, tag="bank", bufs=6)

        def transpose_dy(u):
            words = dy_plain[u][:].rearrange("p j f -> p (j f)").bitcast(F32)
            words_of_slot = HEAD_DIM // 2
            banks = []
            for slot_pair in range(2):
                bank = new_bank("dyT_bank")
                by_slot = bank[:].rearrange("q (a v p) -> q a v p", a=2, v=2)
                for a in range(2):
                    j = 2 * slot_pair + a
                    for v in range(2):
                        nc.tensor.transpose(by_slot[:, a, v, :], words[:, words_of_slot * j + v : words_of_slot * (j + 1) : 2], identity[:])
                banks.append(bank)
            dyT_banks[u] = banks

        def copy_dyT(u):
            grouped = sbuf.tile([P, TOKENS, PACK], BF16, name="dyT_grouped", tag="dyT_grouped", bufs=2, align_bytes=64)
            words = grouped[:].rearrange("q n t -> q (n t)").bitcast(F32).rearrange("q (j p v) -> q j p v", j=PACK, v=2)
            for slot_pair in range(2):
                nc.scalar.copy(out=words[:, 2 * slot_pair : 2 * slot_pair + 2, :, :], in_=dyT_banks[u][slot_pair][:].rearrange("q (a v p) -> q a p v", a=2, v=2))
            dyT_grouped[u] = grouped

        def quantize_dyT(u):
            codes = sbuf.tile([P, TOKENS], U32, name="dyT_codes", tag="dyT_codes", bufs=2, align_bytes=64)
            scales = sbuf.tile([P, TOKENS], U8, name="dyT_scales", tag="dyT_scales", bufs=2, align_bytes=64)
            nc.vector.quantize_mx(out=codes[:].bitcast(E5M2_X4), scales=scales[:], in_=dyT_grouped[u][:].rearrange("q n t -> q (n t)"))
            dyT_mx[u] = (codes, scales)

        def multiply_out_0(u):
            h = units[u][2]
            codes, scales = dyT_mx[u]
            banks = []
            for j in range(PACK):
                bank = new_bank("out_0_bank")
                nc.tensor.matmul_mx(
                    out=bank[:],
                    lhsT=codes[:, P * j : P * (j + 1)].bitcast(E5M2_X4),
                    lhsT_scale=scales[:, P * j : P * (j + 1)],
                    rhs=w_codes[:, h, :].bitcast(E4M3_X4),
                    rhs_scale=w_scales[:, h, :],
                    start=True,
                    stop=True,
                )
                banks.append(bank)
            out_0_banks[u] = banks

        def new_staging(name):
            return sbuf.tile([P, 4, BANK_F32], F32, name=name, tag="staging", bufs=2)

        def store_out_0(u):
            e, i, h = units[u]
            staging = new_staging("out_0_staging")
            for j in range(PACK):
                nc.scalar.copy(out=staging[:, j, :], in_=out_0_banks[u][j][:])
            nc.sync.dma_start(
                out=out_0[TOKENS * i : TOKENS * (i + 1), HEAD_DIM * h : HEAD_DIM * (h + 1)].rearrange("(p j) d -> p j d", j=PACK), in_=staging[:]
            )

        def multiply_out_1(chunk, f_tile):
            dy_codes, dy_scales = dy_mx[chunk]
            x_codes, x_scales = x_mx[chunk]
            bank = new_bank("out_1_bank")
            for i in range(2):
                nc.tensor.matmul_mx(
                    out=bank[:],
                    lhsT=dy_codes[:, i, P * f_tile : P * (f_tile + 1)].bitcast(E5M2_X4),
                    lhsT_scale=dy_scales[:, i, P * f_tile : P * (f_tile + 1)],
                    rhs=x_codes[:, i, :].bitcast(E4M3_X4),
                    rhs_scale=x_scales[:, i, :],
                    start=(i == 0),
                    stop=(i == 1),
                )
            out_1_banks[(chunk, f_tile)] = bank

        def out_1_of_chunk(chunk):
            f0 = HEAD_DIM * row_of_chunk(chunk)
            return out_1_rows[f0 : f0 + HEAD_DIM, :].rearrange("(t p) d -> p t d", p=P)

        def store_out_1(chunk):
            staging = new_staging("out_1_staging")
            for f_tile in range(4):
                nc.scalar.copy(out=staging[:, f_tile, :], in_=out_1_banks[(chunk, f_tile)][:])
            nc.sync.dma_start(out=out_1_of_chunk(chunk), in_=staging[:])

        def finish_last_unit(u):
            chunk = chunk_of(u)
            quantize_x(u)
            new_dy_grouped(u)
            for k in range(4):
                times_c_on_vector(u, P * k, P * (k + 1))
                if k > 0:
                    quantize_dy(u, P * (k - 1), P * k)
                    multiply_out_1(chunk, k - 1)
            quantize_dy(u, P * 3, P * 4)
            multiply_out_1(chunk, 3)
            staging = new_staging("out_1_staging")
            for f_tile in range(4):
                if f_tile % 2 == 0:
                    nc.scalar.copy(out=staging[:, f_tile, :], in_=out_1_banks[(chunk, f_tile)][:])
                else:
                    nc.vector.tensor_copy(out=staging[:, f_tile, :], in_=out_1_banks[(chunk, f_tile)][:])
                nc.sync.dma_start(out=out_1_of_chunk(chunk)[:, f_tile : f_tile + 1, :], in_=staging[:, f_tile : f_tile + 1, :])

        unstored_chunks = []
        for s in range(-3, n_units):
            if is_unit(s + 3):
                load_y_and_g(s + 3)
            if is_unit(s + 2):
                load_x(s + 2)
            if s == 0:
                load_w(0)
                load_w(1)

            new_chunks = [chunk for chunk in range(2, 6) if s == first_unit(chunk) - 1]
            if is_unit(s + 1):
                tanh_and_silu(s + 1)
            for chunk in new_chunks:
                spread_c(chunk)
            if is_unit(s):
                interleave_x(s)
            for chunk in new_chunks:
                copy_c_for_gpsimd(chunk)
            for chunk in unstored_chunks:
                store_out_1(chunk)
            unstored_chunks = []
            if is_expert0(s - 1):
                copy_dyT(s - 1)
            if is_expert0(s - 3):
                store_out_0(s - 3)

            if is_unit(s):
                times_g(s)
            if s == 0:
                make_c_rows()
                for chunk in range(2):
                    spread_c(chunk)
                for chunk in range(2):
                    copy_c_for_gpsimd(chunk)
            quantised = []
            if is_expert0(s - 2):
                quantised.append(s - 2)
            if is_later_expert(s - 1):
                quantised.append(s - 1)
            for u in quantised:
                quantize_dy(u)
            if is_unit(s - 1):
                quantize_x(s - 1)
            for u in quantised:
                if closes_chunk(u):
                    for f_tile in range(4):
                        multiply_out_1(chunk_of(u), f_tile)
                    unstored_chunks.append(chunk_of(u))
            if is_unit(s):
                times_silu(s)
            if s == last:
                for chunk in unstored_chunks:
                    store_out_1(chunk)
                unstored_chunks = []
                finish_last_unit(s)
            elif is_unit(s):
                if is_expert0(s):
                    new_dy_plain(s)
                else:
                    new_dy_grouped(s)
                times_c_on_gpsimd(s)
                times_c_on_vector(s, 0, VECTOR_COLS)
                if is_expert0(s):
                    transpose_dy(s)
            if s in (1, 2):
                interleave_w(s - 1)
            if is_expert0(s - 1):
                interleave_dy(s - 1)
            if s in (2, 3):
                quantize_w(s - 2)
            if is_expert0(s - 2):
                quantize_dyT(s - 2)
                multiply_out_0(s - 2)
